import numpy as np
import ml_dtypes


def mxq(x, axis, fmt="e4m3"):
    dtype, down = {"e4m3": (ml_dtypes.float8_e4m3fn, 7), "e5m2": (ml_dtypes.float8_e5m2, 14)}[fmt]
    v = np.moveaxis(np.asarray(x, np.float32).astype(ml_dtypes.bfloat16).astype(np.float64), axis, -1)
    blocks = v.reshape(v.shape[:-1] + (-1, 32))
    amax = np.abs(blocks).max(-1, keepdims=True)
    byte = np.maximum(np.where(amax > 0, np.frexp(amax)[1] - 1 + 127, 0) - down, 1)
    scale = np.exp2(byte - 127.0)
    codes = (blocks / scale).astype(np.float32).astype(dtype).astype(np.float64)
    return np.moveaxis((codes * scale).reshape(v.shape), -1, axis)


WIDE = False


def mx_kscale(k):
    if not WIDE:
        return np.ones(k)
    levels = np.array([10, -10, 5, -5, 0])
    a = np.random.permutation(np.resize(levels, k // 512 * 4)).reshape(k // 512, 4)
    idx = np.arange(k)
    return np.exp2(a[idx // 512, idx % 128 // 32])


BF16 = ml_dtypes.bfloat16


def bf(x):
    return np.asarray(x, np.float32).astype(BF16)


def f64(x):
    return np.asarray(x).astype(np.float64)


B, I, O, G = 512, 512, 512, 32


def setup_inputs():
    s = mx_kscale(I * G).reshape(I, G)[:, 0]
    a = np.log2(s / s.max())
    d = np.sqrt(np.abs(a) * np.log(2.0) / 20.0)
    u = np.random.random((B, I))
    x = np.where(a < 0, 1.0 + d + 0.1 * (u - 0.5), u)
    w = np.random.standard_normal((I * G, O)) * 2.0 / np.sqrt(I * G) * np.repeat(np.exp2(-a), G)[:, None]
    return {"x": bf(x), "spline_weight": bf(w), "base_weight": bf(np.random.standard_normal((O, I)) / np.sqrt(I)),
            "grid": bf(np.linspace(0.0, 1.0, G))}


def reference(x, spline_weight, base_weight, grid):
    x = f64(x)
    base_output = x @ f64(base_weight).T
    basis = np.exp(-20.0 * (x[:, :, None] - f64(grid)[None, None, :]) ** 2)
    basis = basis.reshape(x.shape[0], -1)
    return base_output + (mxq(basis, 1, "e4m3") @ mxq(f64(spline_weight), 0, "e4m3"))

@@ -1,0 +1,443 @@
+from contextlib import ExitStack
+
+import concourse.mybir as mybir
+from concourse.masks import make_identity
+
+BF16 = mybir.dt.bfloat16
+F32 = mybir.dt.float32
+U32 = mybir.dt.uint32
+U8 = mybir.dt.uint8
+FP8X4 = mybir.dt.float8_e4m3fn_x4
+ALU = mybir.AluOpType
+ACT = mybir.ActivationFunctionType
+AX = mybir.AxisListType
+
+P = 128
+B = 512
+I = 512
+O = 512
+G = 32
+NBT = B // P
+ROUNDS = 16
+NCOL = 1024
+PE_ROUNDS = 4
+NR = ROUNDS - PE_ROUNDS
+PF0 = I - 32 * PE_ROUNDS
+NPP = 2 * PE_ROUNDS
+
+FLOPS = 2 * B * I * G * O + 2 * B * I * O
+
+V_PLANES = [(3,)] * NR
+XR_ON_GPSIMD = False
+
+
+def tile_rbfkanlayer_kernel(tc, x, spline_weight, base_weight, grid, out):
+    nc = tc.nc
+    with ExitStack() as ctx:
+        const = ctx.enter_context(tc.tile_pool(name="const", bufs=1))
+        wraw = ctx.enter_context(tc.tile_pool(name="wraw", bufs=4))
+        work = ctx.enter_context(tc.tile_pool(name="work", bufs=3))
+        small = ctx.enter_context(tc.tile_pool(name="small", bufs=2))
+        psacc = ctx.enter_context(tc.psum_pool(name="psacc", bufs=1))
+        ps2 = ctx.enter_context(tc.psum_pool(name="ps2", bufs=2))
+        ps1 = ctx.enter_context(tc.psum_pool(name="ps1", bufs=1))
+        ctx.enter_context(tc.manual_schedule())
+
+        ident = const.tile([P, P], BF16)
+        gb = const.tile([P, G], BF16)
+        x_sb = const.tile([P, NBT, I], BF16)
+        bw_sb = const.tile([P, NBT, I], BF16)
+        gneg = const.tile([P, 4], F32)
+        base_sb = const.tile([P, NBT, O], F32)
+        xT = const.tile([P, 4, B], BF16)
+        bwT = const.tile([P, 4, O], BF16)
+        zb = const.tile([P, NBT, NPP, P], BF16)
+        q32 = const.tile([P, NBT, NPP, 16], F32)
+        lmat = const.tile([P, 4, 16, 8], BF16)
+        acc = [psacc.tile([P, O], F32, name="acc%d" % bt) for bt in range(NBT)]
+        xp = x_sb[:, :, PF0:I].rearrange("p t (c i) -> p t c i", i=16)
+
+        wr_t = {}
+        wq_t = {}
+        xr_t = {}
+        xs_t = {}
+        xv_t = {}
+        sq_t = {}
+        bg_t = {}
+        bq_t = {}
+        zt_t = {}
+        arg_t = {}
+
+        def grid_scalars():
+            mask8 = const.tile([P, 8], F32, name="mask8")
+            nc.vector.tensor_reduce(
+                out=mask8[:], in_=ident[:].rearrange("p (a q) -> p q a", q=8), axis=AX.X, op=ALU.add
+            )
+            prod = const.tile([P, 4, 8], F32, name="prod")
+            nc.vector.tensor_tensor(
+                out=prod[:],
+                in0=gb[:].rearrange("p (q t) -> p t q", t=4),
+                in1=mask8[:].unsqueeze(1).to_broadcast([P, 4, 8]),
+                op=ALU.mult,
+            )
+            gsel = const.tile([P, 4], F32, name="gsel")
+            nc.vector.tensor_reduce(out=gsel[:], in_=prod[:], axis=AX.X, op=ALU.add)
+            nc.vector.tensor_scalar(
+                out=gneg[:], in0=gsel[:], scalar1=-1.0, scalar2=None, op0=ALU.mult
+            )
+
+        def exponent_rows():
+            nc.gpsimd.memset(zb[:], 0.0)
+            nc.gpsimd.memset(zb[:, :, :, 16:19], 1.0)
+            nc.gpsimd.tensor_copy(out=zb[:, :, :, 0:16], in_=xp)
+            nc.gpsimd.tensor_copy(out=zb[:, :, :, 32:48], in_=xp)
+            nc.gpsimd.tensor_tensor(out=q32[:], in0=xp, in1=xp, op=ALU.mult)
+            nc.gpsimd.tensor_copy(out=zb[:, :, :, 64:80], in_=q32[:])
+            nc.gpsimd.tensor_tensor(
+                out=zb[:, :, :, 96:112], in0=q32[:], in1=zb[:, :, :, 64:80], op=ALU.subtract
+            )
+
+        def exponent_weights():
+            gf = const.tile([P, G], F32, name="gf")
+            nc.vector.tensor_copy(out=gf[:], in_=gb[:])
+            g2 = const.tile([P, G], F32, name="g2")
+            nc.vector.tensor_tensor(out=g2[:], in0=gf[:], in1=gf[:], op=ALU.mult)
+            cc = const.tile([P, G], F32, name="cc")
+            nc.vector.tensor_scalar(out=cc[:], in0=g2[:], scalar1=-20.0, scalar2=None, op0=ALU.mult)
+            c1 = const.tile([P, G], BF16, name="c1")
+            nc.vector.tensor_copy(out=c1[:], in_=cc[:])
+            r1 = const.tile([P, G], F32, name="r1")
+            nc.vector.tensor_tensor(out=r1[:], in0=cc[:], in1=c1[:], op=ALU.subtract)
+            c2 = const.tile([P, G], BF16, name="c2")
+            nc.vector.tensor_copy(out=c2[:], in_=r1[:])
+            c3 = const.tile([P, G], F32, name="c3")
+            nc.vector.tensor_tensor(out=c3[:], in0=r1[:], in1=c2[:], op=ALU.subtract)
+            e3 = const.tile([P, 3], F32, name="e3")
+            nc.vector.tensor_copy(out=e3[:], in_=ident[:, 16:19])
+            pa = const.tile([P, G], F32, name="pa")
+            nc.vector.tensor_scalar(out=pa[:], in0=c1[:], scalar1=e3[:, 0:1], scalar2=None, op0=ALU.mult)
+            pb = const.tile([P, G], F32, name="pb")
+            nc.vector.scalar_tensor_tensor(
+                out=pb[:], in0=c2[:], scalar=e3[:, 1:2], in1=pa[:], op0=ALU.mult, op1=ALU.add
+            )
+            pc = const.tile([P, G], F32, name="pc")
+            nc.vector.scalar_tensor_tensor(
+                out=pc[:], in0=c3[:], scalar=e3[:, 2:3], in1=pb[:], op0=ALU.mult, op1=ALU.add
+            )
+            alpha = const.tile([P, 1], F32, name="alpha")
+            nc.vector.memset(alpha[0:32, :], 32.0)
+            nc.vector.memset(alpha[32:64, :], 8.0)
+            nc.vector.memset(alpha[64:128, :], 0.0)
+            beta = const.tile([P, 1], F32, name="beta")
+            nc.vector.memset(beta[0:64, :], 0.0)
+            nc.vector.memset(beta[64:128, :], -20.0)
+            ag = const.tile([P, G], F32, name="ag")
+            nc.vector.tensor_scalar(
+                out=ag[:], in0=gf[:], scalar1=alpha[:], scalar2=beta[:], op0=ALU.mult, op1=ALU.add
+            )
+            msum = const.tile([P, 16], F32, name="msum")
+            nc.vector.tensor_reduce(
+                out=msum[:],
+                in_=ident[:].rearrange("p (g h i) -> p h i g", g=4, h=2)[:, 0],
+                axis=AX.X,
+                op=ALU.add,
+            )
+            shape = [P, 4, 16, 8]
+            tmp = const.tile(shape, F32, name="tmp")
+            nc.vector.tensor_tensor(
+                out=tmp[:],
+                in0=ag[:].rearrange("p (q t) -> p t q", t=4).unsqueeze(2).to_broadcast(shape),
+                in1=msum[:].unsqueeze(1).unsqueeze(3).to_broadcast(shape),
+                op=ALU.mult,
+            )
+            nc.vector.tensor_tensor(
+                out=lmat[:],
+                in0=tmp[:],
+                in1=pc[:].rearrange("p (q t) -> p t q", t=4).unsqueeze(2).to_broadcast(shape),
+                op=ALU.add,
+            )
+
+        ex_t = {}
+
+        def base_pe(j):
+            if j < 4:
+                src = (x_sb, bw_sb)[j // 2]
+                h = j % 2
+                tp = ps1.tile([P, 2, 512], BF16, tag="ex", name="tp")
+                for k in range(2):
+                    for bt in range(NBT):
+                        nc.tensor.transpose(
+                            tp[:, k, bt * P : (bt + 1) * P],
+                            src[:, bt, (2 * h + k) * P : (2 * h + k + 1) * P],
+                            ident[:],
+                        )
+                ex_t[j] = tp
+            else:
+                bt = j - 4
+                bp = ps1.tile([P, O], F32, tag="ex", name="bp")
+                for it in range(4):
+                    nc.tensor.matmul(
+                        out=bp[:],
+                        lhsT=xT[:, it, bt * P : (bt + 1) * P],
+                        rhs=bwT[:, it, :],
+                        start=(it == 0),
+                        stop=(it == 3),
+                    )
+                ex_t[j] = bp
+
+        def base_v(j):
+            if j < 4:
+                dst = (xT, bwT)[j // 2]
+                h = j % 2
+                nc.vector.tensor_copy(out=dst[:, 2 * h : 2 * h + 2, :], in_=ex_t[j][:])
+            else:
+                nc.vector.tensor_copy(out=base_sb[:, j - 4, :], in_=ex_t[j][:])
+
+        def w_load(r):
+            wr = wraw.tile([P, 2, 4, O], BF16, name="wr")
+            nc.sync.dma_start(
+                out=wr[:],
+                in_=spline_weight[r * 1024 : (r + 1) * 1024, :].rearrange(
+                    "(c p j) o -> p c j o", c=2, p=P, j=4
+                ),
+            )
+            wr_t[r] = wr
+
+        wg_t = {}
+
+        def w_group(r, c):
+            if c == 0:
+                wg_t[r] = work.tile([P, 2, O, 4], BF16, align_bytes=64, name="wg")
+            nc.vector.tensor_copy(
+                out=wg_t[r][:, c].rearrange("p (c i) t -> p c t i", i=4),
+                in_=wr_t[r][:, c].rearrange("p t (c i) -> p c t i", i=4),
+            )
+
+        def w_quant(r):
+            wc = work.tile([P, NCOL], U32, align_bytes=64, name="wc")
+            ws = work.tile([P, NCOL], U8, align_bytes=64, name="ws")
+            nc.vector.quantize_mx(
+                out=wc[:].bitcast(FP8X4),
+                scales=ws[:],
+                in_=wg_t[r][:].rearrange("p c o t -> p (c o t)"),
+            )
+            wq_t[r] = (wc, ws)
+
+        def mx(r, c, bt, lo):
+            bc, bs = bq_t[r]
+            wc, ws = wq_t[r]
+            nc.tensor.matmul_mx(
+                out=acc[bt][:],
+                lhsT=bc[:, lo : lo + P].bitcast(FP8X4),
+                lhsT_scale=bs[:, lo : lo + P],
+                rhs=wc[:, c * 512 : (c + 1) * 512].bitcast(FP8X4),
+                rhs_scale=ws[:, c * 512 : (c + 1) * 512],
+                start=(r == 0 and c == 0),
+                stop=(r == ROUNDS - 1 and c == 1),
+            )
+
+        def x_repeat(r):
+            xr = work.tile([P, NBT, 32, 8], BF16, name="xr")
+            src = x_sb[:, :, r * 32 : (r + 1) * 32].unsqueeze(3).to_broadcast([P, NBT, 32, 8])
+            if XR_ON_GPSIMD:
+                nc.gpsimd.tensor_scalar(
+                    out=xr[:], in0=src, scalar1=1.0, scalar2=0.0, op0=ALU.mult, op1=ALU.add
+                )
+            else:
+                nc.vector.tensor_copy(out=xr[:], in_=src)
+            xr_t[r] = xr
+
+        def x_transpose(r):
+            xs_t[r] = ps2.tile([P, 2, 512], BF16, tag="xs", name="xs")
+            dsts = [xs_t[r]]
+            if V_PLANES[r]:
+                xv_t[r] = ps1.tile([P, 2, 512], BF16, tag="xv", name="xv")
+                dsts.append(xv_t[r])
+            for dst in dsts:
+                for c in range(2):
+                    for bt in range(NBT):
+                        nc.tensor.transpose(
+                            dst[:, c, bt * P : (bt + 1) * P],
+                            xr_t[r][:, bt, 16 * c : 16 * c + 16, :].rearrange("p a b -> p (a b)"),
+                            ident[:],
+                        )
+
+        def squares_v(r):
+            sq_t[r] = work.tile([P, 4, NCOL], F32, name="sq")
+            for t in V_PLANES[r]:
+                d = small.tile([P, NCOL], F32, name="d")
+                nc.vector.tensor_scalar(
+                    out=d[:],
+                    in0=xv_t[r][:].rearrange("p c b -> p (c b)"),
+                    scalar1=gneg[:, t : t + 1],
+                    scalar2=None,
+                    op0=ALU.add,
+                )
+                nc.vector.tensor_tensor(out=sq_t[r][:, t, :], in0=d[:], in1=d[:], op=ALU.mult)
+
+        def squares_s(r):
+            for t in range(4):
+                if t not in V_PLANES[r]:
+                    nc.scalar.activation(
+                        out=sq_t[r][:, t, :],
+                        in_=xs_t[r][:].rearrange("p c b -> p (c b)"),
+                        func=ACT.Square,
+                        bias=gneg[:, t : t + 1],
+                        scale=1.0,
+                    )
+
+        def exp_s(r):
+            bg = work.tile([P, NCOL, 4], BF16, align_bytes=64, name="bg")
+            nc.scalar.activation(
+                out=bg[:].rearrange("p (c i) t -> p c t i", i=4),
+                in_=sq_t[r][:].rearrange("p t (c i) -> p c t i", i=4),
+                func=ACT.Exp,
+                scale=-20.0,
+            )
+            bg_t[r] = bg
+
+        def b_tiles(r):
+            bc = work.tile([P, NCOL], U32, align_bytes=64, name="bc")
+            bs = work.tile([P, NCOL], U8, align_bytes=64, name="bs")
+            bq_t[r] = (bc, bs)
+
+        def b_quant(r, lo, n):
+            bc, bs = bq_t[r]
+            nc.vector.quantize_mx(
+                out=bc[:, lo : lo + n].bitcast(FP8X4),
+                scales=bs[:, lo : lo + n],
+                in_=bg_t[r][:, lo : lo + n, :].rearrange("p n t -> p (n t)"),
+            )
+
+        def z_transpose(r):
+            ztp = ps1.tile([P, 2, 512], BF16, tag="ex", name="ztp")
+            for c in range(2):
+                for bt in range(NBT):
+                    nc.tensor.transpose(
+                        ztp[:, c, bt * P : (bt + 1) * P], zb[:, bt, 2 * (r - NR) + c, :], ident[:]
+                    )
+            ex_t[r] = ztp
+
+        def z_copy(r):
+            zt = work.tile([P, 2, 512], BF16, name="zt")
+            nc.scalar.copy(out=zt[:], in_=ex_t[r][:])
+            zt_t[r] = zt
+
+        def arg_pe(v):
+            r = NR + v // 8
+            bt = (v % 8) // 2
+            c = v % 2
+            if v % 3 == 2:
+                arg = ps1.tile([P, 4, P], F32, tag="xv", name="arg")
+            else:
+                arg = ps2.tile([P, 4, P], F32, tag="xs", name="arg")
+            for t in range(4):
+                nc.tensor.matmul(
+                    out=arg[:, t, :],
+                    lhsT=lmat[:, t].rearrange("p a b -> p (a b)"),
+                    rhs=zt_t[r][:, c, bt * P : (bt + 1) * P],
+                    start=True,
+                    stop=True,
+                )
+            arg_t[v] = arg
+
+        def arg_exp(v):
+            r = NR + v // 8
+            lo = ((v % 8) // 2) * 256 + (v % 2) * P
+            nc.scalar.activation(
+                out=bg_t[r][:, lo : lo + P, :],
+                in_=arg_t[v][:].rearrange("p t n -> p n t"),
+                func=ACT.Exp,
+            )
+
+        make_identity(nc, ident[:])
+        nc.sync.dma_start(out=gb[:], in_=grid.partition_broadcast(P))
+        nc.sync.dma_start(out=x_sb[:], in_=x.rearrange("(t p) i -> p t i", p=P))
+        for r in range(4):
+            w_load(r)
+        nc.sync.dma_start(out=bw_sb[:], in_=base_weight.rearrange("(t p) i -> p t i", p=P))
+        warm = const.tile([P, 1], F32)
+        nc.vector.memset(warm[:], 0.0)
+        warm2 = const.tile([P, 1], F32)
+        nc.scalar.activation(out=warm2[:], in_=warm[:], func=ACT.Exp)
+        grid_scalars()
+        x_repeat(0)
+        x_transpose(0)
+        x_repeat(1)
+        exponent_rows()
+        exponent_weights()
+        squares_v(0)
+
+        for s in range(NR):
+            if s + 1 < NR:
+                x_transpose(s + 1)
+            else:
+                z_transpose(NR)
+            squares_s(s)
+            if 1 <= s <= 8:
+                base_pe(s - 1)
+            if s == NR - 1:
+                z_copy(NR)
+            w_group(s, 0)
+            w_group(s, 1)
+            if s >= 1:
+                b_tiles(s - 1)
+                b_quant(s - 1, 0, NCOL)
+                for c in range(2):
+                    for bt in range(NBT):
+                        mx(s - 1, c, bt, c * 512 + bt * P)
+            if s + 1 < NR:
+                squares_v(s + 1)
+            else:
+                w_group(s + 1, 0)
+                w_group(s + 1, 1)
+            w_quant(s)
+            if 1 <= s <= 8:
+                base_v(s - 1)
+            if s + 2 < NR:
+                x_repeat(s + 2)
+            if s == NR - 1:
+                w_quant(s + 1)
+            exp_s(s)
+            if s + 4 < ROUNDS:
+                w_load(s + 4)
+
+        NU = 8 * PE_ROUNDS
+        for v in range(3):
+            arg_pe(v)
+        for r in range(NR, ROUNDS):
+            last = r == ROUNDS - 1
+            bg_t[r] = work.tile([P, NCOL, 4], BF16, align_bytes=64, name="bg")
+            if not last:
+                z_transpose(r + 1)
+            if r == NR:
+                b_tiles(r - 1)
+                b_quant(r - 1, 0, NCOL)
+                for c in range(2):
+                    for bt in range(NBT):
+                        mx(r - 1, c, bt, c * 512 + bt * P)
+            b_tiles(r)
+            for bt in range(NBT):
+                for c in range(2):
+                    v = (r - NR) * 8 + bt * 2 + c
+                    arg_exp(v)
+                    if v + 3 < NU:
+                        arg_pe(v + 3)
+                if not last and bt == 1:
+                    z_copy(r + 1)
+                if not last and bt < 2:
+                    w_group(r + 1, bt)
+                if not last and bt == 2:
+                    w_quant(r + 1)
+                b_quant(r, bt * 256, 256)
+                for c in range(2):
+                    mx(r, c, bt, bt * 256 + c * P)
+                if last and bt >= 1:
+                    res = small.tile([P, O], F32, name="res")
+                    nc.vector.tensor_tensor(
+                        out=res[:], in0=acc[bt - 1][:], in1=base_sb[:, bt - 1, :], op=ALU.add
+                    )
+                    nc.sync.dma_start(out=out[(bt - 1) * P : bt * P, :], in_=res[:])
+        res = small.tile([P, O], F32, name="res")
+        nc.vector.tensor_tensor(out=res[:], in0=acc[3][:], in1=base_sb[:, 3, :], op=ALU.add)
+        nc.sync.dma_start(out=out[3 * P : 4 * P, :], in_=res[:])

@@ -28,7 +28,7 @@ NPP = 2 * PE_ROUNDS
 FLOPS = 2 * B * I * G * O + 2 * B * I * O
 
 V_PLANES = [(3,)] * NR
-XR_ON_GPSIMD = False
+XR_ON_GPSIMD = True
 
 
 def tile_rbfkanlayer_kernel(tc, x, spline_weight, base_weight, grid, out):
@@ -86,16 +86,23 @@ def tile_rbfkanlayer_kernel(tc, x, spline_weight, base_weight, grid, out):
                 out=gneg[:], in0=gsel[:], scalar1=-1.0, scalar2=None, op0=ALU.mult
             )
 
-        def exponent_rows():
-            nc.gpsimd.memset(zb[:], 0.0)
-            nc.gpsimd.memset(zb[:, :, :, 16:19], 1.0)
-            nc.gpsimd.tensor_copy(out=zb[:, :, :, 0:16], in_=xp)
-            nc.gpsimd.tensor_copy(out=zb[:, :, :, 32:48], in_=xp)
-            nc.gpsimd.tensor_tensor(out=q32[:], in0=xp, in1=xp, op=ALU.mult)
-            nc.gpsimd.tensor_copy(out=zb[:, :, :, 64:80], in_=q32[:])
-            nc.gpsimd.tensor_tensor(
-                out=zb[:, :, :, 96:112], in0=q32[:], in1=zb[:, :, :, 64:80], op=ALU.subtract
-            )
+        def exponent_rows(step):
+            if step == 0:
+                nc.gpsimd.memset(zb[:], 0.0)
+            if step == 1:
+                nc.gpsimd.memset(zb[:, :, :, 16:19], 1.0)
+            if step == 2:
+                nc.gpsimd.tensor_copy(out=zb[:, :, :, 0:16], in_=xp)
+            if step == 3:
+                nc.gpsimd.tensor_copy(out=zb[:, :, :, 32:48], in_=xp)
+            if step == 4:
+                nc.gpsimd.tensor_tensor(out=q32[:], in0=xp, in1=xp, op=ALU.mult)
+            if step == 5:
+                nc.gpsimd.tensor_copy(out=zb[:, :, :, 64:80], in_=q32[:])
+            if step == 6:
+                nc.gpsimd.tensor_tensor(
+                    out=zb[:, :, :, 96:112], in0=q32[:], in1=zb[:, :, :, 64:80], op=ALU.subtract
+                )
 
         def exponent_weights():
             gf = const.tile([P, G], F32, name="gf")
@@ -239,7 +246,7 @@ def tile_rbfkanlayer_kernel(tc, x, spline_weight, base_weight, grid, out):
         def x_repeat(r):
             xr = work.tile([P, NBT, 32, 8], BF16, name="xr")
             src = x_sb[:, :, r * 32 : (r + 1) * 32].unsqueeze(3).to_broadcast([P, NBT, 32, 8])
-            if XR_ON_GPSIMD:
+            if XR_ON_GPSIMD and r >= 2:
                 nc.gpsimd.tensor_scalar(
                     out=xr[:], in0=src, scalar1=1.0, scalar2=0.0, op0=ALU.mult, op1=ALU.add
                 )
@@ -364,7 +371,6 @@ def tile_rbfkanlayer_kernel(tc, x, spline_weight, base_weight, grid, out):
         x_repeat(0)
         x_transpose(0)
         x_repeat(1)
-        exponent_rows()
         exponent_weights()
         squares_v(0)
 
@@ -396,6 +402,8 @@ def tile_rbfkanlayer_kernel(tc, x, spline_weight, base_weight, grid, out):
                 base_v(s - 1)
             if s + 2 < NR:
                 x_repeat(s + 2)
+            if s < 7:
+                exponent_rows(s)
             if s == NR - 1:
                 w_quant(s + 1)
             exp_s(s)

@@ -270,7 +270,7 @@ def tile_rbfkanlayer_kernel(tc, x, spline_weight, base_weight, grid, out):
                         )
 
         def squares_v(r):
-            sq_t[r] = work.tile([P, 4, NCOL], F32, name="sq")
+            sq_t[r] = work.tile([P, NCOL // 8, 4, 8], F32, name="sq")
             for t in V_PLANES[r]:
                 d = small.tile([P, NCOL], F32, name="d")
                 nc.vector.tensor_scalar(
@@ -280,14 +280,15 @@ def tile_rbfkanlayer_kernel(tc, x, spline_weight, base_weight, grid, out):
                     scalar2=None,
                     op0=ALU.add,
                 )
-                nc.vector.tensor_tensor(out=sq_t[r][:, t, :], in0=d[:], in1=d[:], op=ALU.mult)
+                dv = d[:].rearrange("p (c i) -> p c i", i=8)
+                nc.vector.tensor_tensor(out=sq_t[r][:, :, t, :], in0=dv, in1=dv, op=ALU.mult)
 
         def squares_s(r):
             for t in range(4):
                 if t not in V_PLANES[r]:
                     nc.scalar.activation(
-                        out=sq_t[r][:, t, :],
-                        in_=xs_t[r][:].rearrange("p c b -> p (c b)"),
+                        out=sq_t[r][:, :, t, :],
+                        in_=xs_t[r][:].rearrange("p c (b i) -> p (c b) i", i=8),
                         func=ACT.Square,
                         bias=gneg[:, t : t + 1],
                         scale=1.0,
@@ -296,8 +297,8 @@ def tile_rbfkanlayer_kernel(tc, x, spline_weight, base_weight, grid, out):
         def exp_s(r):
             bg = work.tile([P, NCOL, 4], BF16, align_bytes=64, name="bg")
             nc.scalar.activation(
-                out=bg[:].rearrange("p (c i) t -> p c t i", i=4),
-                in_=sq_t[r][:].rearrange("p t (c i) -> p c t i", i=4),
+                out=bg[:].rearrange("p (c i) t -> p c t i", i=8),
+                in_=sq_t[r][:],
                 func=ACT.Exp,
                 scale=-20.0,
             )

@@ -27,7 +27,7 @@ NPP = 2 * PE_ROUNDS
 
 FLOPS = 2 * B * I * G * O + 2 * B * I * O
 
-V_PLANES = [(3,)] * NR
+V_PLANES = [()] * NR
 XR_ON_GPSIMD = True
 
 

@@ -20,15 +20,15 @@ G = 32
 NBT = B // P
 ROUNDS = 16
 NCOL = 1024
-PE_ROUNDS = 4
-NR = ROUNDS - PE_ROUNDS
-PF0 = I - 32 * PE_ROUNDS
-NPP = 2 * PE_ROUNDS
+PR = (0, 1, 2, 15)
+N0 = 3
+NR = 12
 
 FLOPS = 2 * B * I * G * O + 2 * B * I * O
 
-V_PLANES = [()] * NR
-XR_ON_GPSIMD = True
+V_PLANES = [(2, 3)] + [(3,)] * (NR - 1)
+MX_PLAN = {0: (0, 1), 1: (2, 3)}
+X_CHUNKS = ((0, 4), (4, 12), (12, 24))
 
 
 def tile_rbfkanlayer_kernel(tc, x, spline_weight, base_weight, grid, out):
@@ -36,8 +36,8 @@ def tile_rbfkanlayer_kernel(tc, x, spline_weight, base_weight, grid, out):
     with ExitStack() as ctx:
         const = ctx.enter_context(tc.tile_pool(name="const", bufs=1))
         wraw = ctx.enter_context(tc.tile_pool(name="wraw", bufs=4))
-        work = ctx.enter_context(tc.tile_pool(name="work", bufs=3))
-        small = ctx.enter_context(tc.tile_pool(name="small", bufs=2))
+        work3 = ctx.enter_context(tc.tile_pool(name="work3", bufs=3))
+        work2 = ctx.enter_context(tc.tile_pool(name="work2", bufs=2))
         psacc = ctx.enter_context(tc.psum_pool(name="psacc", bufs=1))
         ps2 = ctx.enter_context(tc.psum_pool(name="ps2", bufs=2))
         ps1 = ctx.enter_context(tc.psum_pool(name="ps1", bufs=1))
@@ -51,28 +51,43 @@ def tile_rbfkanlayer_kernel(tc, x, spline_weight, base_weight, grid, out):
         base_sb = const.tile([P, NBT, O], F32)
         xT = const.tile([P, 4, B], BF16)
         bwT = const.tile([P, 4, O], BF16)
-        zb = const.tile([P, NBT, NPP, P], BF16)
-        q32 = const.tile([P, NBT, NPP, 16], F32)
+        zb = const.tile([P, 4, NBT, 2, P], BF16)
         lmat = const.tile([P, 4, 16, 8], BF16)
+        x_all = const.tile([P, 2 * NR, B], BF16)
         acc = [psacc.tile([P, O], F32, name="acc%d" % bt) for bt in range(NBT)]
-        xp = x_sb[:, :, PF0:I].rearrange("p t (c i) -> p t c i", i=16)
+        scratch = out.bitcast(BF16)[:, 0:B]
 
         wr_t = {}
+        wg_t = {}
         wq_t = {}
-        xr_t = {}
-        xs_t = {}
-        xv_t = {}
         sq_t = {}
         bg_t = {}
         bq_t = {}
         zt_t = {}
         arg_t = {}
+        ex_t = {}
 
-        def grid_scalars():
-            mask8 = const.tile([P, 8], F32, name="mask8")
+        mask8 = const.tile([P, 8], F32)
+        e3 = const.tile([P, 3], F32)
+        msum = const.tile([P, 16], F32)
+        alpha = const.tile([P, 1], F32)
+        beta = const.tile([P, 1], F32)
+        pc = const.tile([P, G], F32)
+        ag = const.tile([P, G], F32)
+
+        def from_identity():
             nc.vector.tensor_reduce(
                 out=mask8[:], in_=ident[:].rearrange("p (a q) -> p q a", q=8), axis=AX.X, op=ALU.add
             )
+            nc.vector.tensor_copy(out=e3[:], in_=ident[:, 16:19])
+            nc.vector.tensor_reduce(
+                out=msum[:],
+                in_=ident[:].rearrange("p (g h i) -> p h i g", g=4, h=2)[:, 0],
+                axis=AX.X,
+                op=ALU.add,
+            )
+
+        def grid_scalars():
             prod = const.tile([P, 4, 8], F32, name="prod")
             nc.vector.tensor_tensor(
                 out=prod[:],
@@ -86,76 +101,43 @@ def tile_rbfkanlayer_kernel(tc, x, spline_weight, base_weight, grid, out):
                 out=gneg[:], in0=gsel[:], scalar1=-1.0, scalar2=None, op0=ALU.mult
             )
 
-        def exponent_rows(step):
-            if step == 0:
-                nc.gpsimd.memset(zb[:], 0.0)
-            if step == 1:
-                nc.gpsimd.memset(zb[:, :, :, 16:19], 1.0)
-            if step == 2:
-                nc.gpsimd.tensor_copy(out=zb[:, :, :, 0:16], in_=xp)
-            if step == 3:
-                nc.gpsimd.tensor_copy(out=zb[:, :, :, 32:48], in_=xp)
-            if step == 4:
-                nc.gpsimd.tensor_tensor(out=q32[:], in0=xp, in1=xp, op=ALU.mult)
-            if step == 5:
-                nc.gpsimd.tensor_copy(out=zb[:, :, :, 64:80], in_=q32[:])
-            if step == 6:
-                nc.gpsimd.tensor_tensor(
-                    out=zb[:, :, :, 96:112], in0=q32[:], in1=zb[:, :, :, 64:80], op=ALU.subtract
-                )
-
-        def exponent_weights():
-            gf = const.tile([P, G], F32, name="gf")
-            nc.vector.tensor_copy(out=gf[:], in_=gb[:])
-            g2 = const.tile([P, G], F32, name="g2")
-            nc.vector.tensor_tensor(out=g2[:], in0=gf[:], in1=gf[:], op=ALU.mult)
+        def exponent_weights(fill):
+            shape = [P, 4, 16, 8]
             cc = const.tile([P, G], F32, name="cc")
-            nc.vector.tensor_scalar(out=cc[:], in0=g2[:], scalar1=-20.0, scalar2=None, op0=ALU.mult)
+            nc.vector.scalar_tensor_tensor(
+                out=cc[:], in0=gb[:], scalar=-20.0, in1=gb[:], op0=ALU.mult, op1=ALU.mult
+            )
+            nc.vector.tensor_scalar(
+                out=ag[:], in0=gb[:], scalar1=alpha[:], scalar2=beta[:], op0=ALU.mult, op1=ALU.add
+            )
             c1 = const.tile([P, G], BF16, name="c1")
             nc.vector.tensor_copy(out=c1[:], in_=cc[:])
-            r1 = const.tile([P, G], F32, name="r1")
-            nc.vector.tensor_tensor(out=r1[:], in0=cc[:], in1=c1[:], op=ALU.subtract)
-            c2 = const.tile([P, G], BF16, name="c2")
-            nc.vector.tensor_copy(out=c2[:], in_=r1[:])
-            c3 = const.tile([P, G], F32, name="c3")
-            nc.vector.tensor_tensor(out=c3[:], in0=r1[:], in1=c2[:], op=ALU.subtract)
-            e3 = const.tile([P, 3], F32, name="e3")
-            nc.vector.tensor_copy(out=e3[:], in_=ident[:, 16:19])
-            pa = const.tile([P, G], F32, name="pa")
-            nc.vector.tensor_scalar(out=pa[:], in0=c1[:], scalar1=e3[:, 0:1], scalar2=None, op0=ALU.mult)
-            pb = const.tile([P, G], F32, name="pb")
-            nc.vector.scalar_tensor_tensor(
-                out=pb[:], in0=c2[:], scalar=e3[:, 1:2], in1=pa[:], op0=ALU.mult, op1=ALU.add
-            )
-            pc = const.tile([P, G], F32, name="pc")
-            nc.vector.scalar_tensor_tensor(
-                out=pc[:], in0=c3[:], scalar=e3[:, 2:3], in1=pb[:], op0=ALU.mult, op1=ALU.add
-            )
-            alpha = const.tile([P, 1], F32, name="alpha")
-            nc.vector.memset(alpha[0:32, :], 32.0)
-            nc.vector.memset(alpha[32:64, :], 8.0)
-            nc.vector.memset(alpha[64:128, :], 0.0)
-            beta = const.tile([P, 1], F32, name="beta")
-            nc.vector.memset(beta[0:64, :], 0.0)
-            nc.vector.memset(beta[64:128, :], -20.0)
-            ag = const.tile([P, G], F32, name="ag")
-            nc.vector.tensor_scalar(
-                out=ag[:], in0=gf[:], scalar1=alpha[:], scalar2=beta[:], op0=ALU.mult, op1=ALU.add
-            )
-            msum = const.tile([P, 16], F32, name="msum")
-            nc.vector.tensor_reduce(
-                out=msum[:],
-                in_=ident[:].rearrange("p (g h i) -> p h i g", g=4, h=2)[:, 0],
-                axis=AX.X,
-                op=ALU.add,
-            )
-            shape = [P, 4, 16, 8]
             tmp = const.tile(shape, F32, name="tmp")
             nc.vector.tensor_tensor(
                 out=tmp[:],
                 in0=ag[:].rearrange("p (q t) -> p t q", t=4).unsqueeze(2).to_broadcast(shape),
                 in1=msum[:].unsqueeze(1).unsqueeze(3).to_broadcast(shape),
                 op=ALU.mult,
+            )
+            r1 = const.tile([P, G], F32, name="r1")
+            nc.vector.tensor_tensor(out=r1[:], in0=cc[:], in1=c1[:], op=ALU.subtract)
+            pa = const.tile([P, G], F32, name="pa")
+            nc.vector.tensor_scalar(out=pa[:], in0=c1[:], scalar1=e3[:, 0:1], scalar2=None, op0=ALU.mult)
+            fill[0]()
+            c2 = const.tile([P, G], BF16, name="c2")
+            nc.vector.tensor_copy(out=c2[:], in_=r1[:])
+            fill[1]()
+            fill[2]()
+            c3 = const.tile([P, G], F32, name="c3")
+            nc.vector.tensor_tensor(out=c3[:], in0=r1[:], in1=c2[:], op=ALU.subtract)
+            pb = const.tile([P, G], F32, name="pb")
+            nc.vector.scalar_tensor_tensor(
+                out=pb[:], in0=c2[:], scalar=e3[:, 1:2], in1=pa[:], op0=ALU.mult, op1=ALU.add
+            )
+            fill[3]()
+            fill[4]()
+            nc.vector.scalar_tensor_tensor(
+                out=pc[:], in0=c3[:], scalar=e3[:, 2:3], in1=pb[:], op0=ALU.mult, op1=ALU.add
             )
             nc.vector.tensor_tensor(
                 out=lmat[:],
@@ -164,13 +146,29 @@ def tile_rbfkanlayer_kernel(tc, x, spline_weight, base_weight, grid, out):
                 op=ALU.add,
             )
 
-        ex_t = {}
+        def z_rows(pi, eng):
+            f0 = 32 * PR[pi]
+            xp = x_sb[:, :, f0 : f0 + 32].rearrange("p t (c i) -> p t c i", i=16)
+            q32 = work2.tile([P, NBT, 2, 16], F32, name="q32")
+            z = zb[:, pi]
+            return [
+                lambda: eng.tensor_tensor(out=q32[:], in0=xp, in1=xp, op=ALU.mult),
+                lambda: eng.tensor_copy(out=z[:, :, :, 0:16], in_=xp),
+                lambda: eng.tensor_copy(out=z[:, :, :, 64:80], in_=q32[:]),
+                lambda: eng.tensor_copy(out=z[:, :, :, 32:48], in_=xp),
+                lambda: eng.tensor_tensor(
+                    out=z[:, :, :, 96:112], in0=q32[:], in1=z[:, :, :, 64:80], op=ALU.subtract
+                ),
+            ]
 
         def base_pe(j):
             if j < 4:
                 src = (x_sb, bw_sb)[j // 2]
                 h = j % 2
-                tp = ps1.tile([P, 2, 512], BF16, tag="ex", name="tp")
+                if j < 2:
+                    tp = ps2.tile([P, 2, 512], BF16, tag="xs", name="tp")
+                else:
+                    tp = ps1.tile([P, 2, 512], BF16, tag="ex", name="tp")
                 for k in range(2):
                     for bt in range(NBT):
                         nc.tensor.transpose(
@@ -210,19 +208,19 @@ def tile_rbfkanlayer_kernel(tc, x, spline_weight, base_weight, grid, out):
             )
             wr_t[r] = wr
 
-        wg_t = {}
-
         def w_group(r, c):
             if c == 0:
-                wg_t[r] = work.tile([P, 2, O, 4], BF16, align_bytes=64, name="wg")
+                wg_t[r] = work2.tile([P, 2, O, 4], BF16, align_bytes=64, name="wg")
             nc.vector.tensor_copy(
                 out=wg_t[r][:, c].rearrange("p (c i) t -> p c t i", i=4),
                 in_=wr_t[r][:, c].rearrange("p t (c i) -> p c t i", i=4),
             )
+            if c == 1 and r + 4 < ROUNDS:
+                w_load(r + 4)
 
         def w_quant(r):
-            wc = work.tile([P, NCOL], U32, align_bytes=64, name="wc")
-            ws = work.tile([P, NCOL], U8, align_bytes=64, name="ws")
+            wc = work3.tile([P, NCOL], U32, align_bytes=64, name="wc", bufs=4)
+            ws = work3.tile([P, NCOL], U8, align_bytes=64, name="ws", bufs=4)
             nc.vector.quantize_mx(
                 out=wc[:].bitcast(FP8X4),
                 scales=ws[:],
@@ -230,7 +228,8 @@ def tile_rbfkanlayer_kernel(tc, x, spline_weight, base_weight, grid, out):
             )
             wq_t[r] = (wc, ws)
 
-        def mx(r, c, bt, lo):
+        def mx(r, c, bt):
+            lo = bt * 256 + c * P if r in PR else c * 512 + bt * P
             bc, bs = bq_t[r]
             wc, ws = wq_t[r]
             nc.tensor.matmul_mx(
@@ -243,70 +242,54 @@ def tile_rbfkanlayer_kernel(tc, x, spline_weight, base_weight, grid, out):
                 stop=(r == ROUNDS - 1 and c == 1),
             )
 
-        def x_repeat(r):
-            xr = work.tile([P, NBT, 32, 8], BF16, name="xr")
-            src = x_sb[:, :, r * 32 : (r + 1) * 32].unsqueeze(3).to_broadcast([P, NBT, 32, 8])
-            if XR_ON_GPSIMD and r >= 2:
-                nc.gpsimd.tensor_scalar(
-                    out=xr[:], in0=src, scalar1=1.0, scalar2=0.0, op0=ALU.mult, op1=ALU.add
-                )
-            else:
-                nc.vector.tensor_copy(out=xr[:], in_=src)
-            xr_t[r] = xr
-
-        def x_transpose(r):
-            xs_t[r] = ps2.tile([P, 2, 512], BF16, tag="xs", name="xs")
-            dsts = [xs_t[r]]
-            if V_PLANES[r]:
-                xv_t[r] = ps1.tile([P, 2, 512], BF16, tag="xv", name="xv")
-                dsts.append(xv_t[r])
-            for dst in dsts:
-                for c in range(2):
-                    for bt in range(NBT):
-                        nc.tensor.transpose(
-                            dst[:, c, bt * P : (bt + 1) * P],
-                            xr_t[r][:, bt, 16 * c : 16 * c + 16, :].rearrange("p a b -> p (a b)"),
-                            ident[:],
-                        )
-
-        def squares_v(r):
-            sq_t[r] = work.tile([P, NCOL // 8, 4, 8], F32, name="sq")
-            for t in V_PLANES[r]:
-                d = small.tile([P, NCOL], F32, name="d")
+        def diff_v(j):
+            sq_t[j] = work3.tile([P, NCOL // 8, 4, 8], F32, name="sq")
+            for t in V_PLANES[j]:
                 nc.vector.tensor_scalar(
-                    out=d[:],
-                    in0=xv_t[r][:].rearrange("p c b -> p (c b)"),
+                    out=sq_t[j][:, :, t, :],
+                    in0=x_all[:, 2 * j : 2 * j + 2, :].rearrange("p c (b i) -> p (c b) i", i=8),
                     scalar1=gneg[:, t : t + 1],
                     scalar2=None,
                     op0=ALU.add,
                 )
-                dv = d[:].rearrange("p (c i) -> p c i", i=8)
-                nc.vector.tensor_tensor(out=sq_t[r][:, :, t, :], in0=dv, in1=dv, op=ALU.mult)
 
-        def squares_s(r):
+        def squares_v(j):
+            planes = V_PLANES[j]
+            dv = sq_t[j][:, :, planes[0] : planes[-1] + 1, :]
+            nc.vector.tensor_tensor(out=dv, in0=dv, in1=dv, op=ALU.mult)
+
+        def squares_s(j):
             for t in range(4):
-                if t not in V_PLANES[r]:
+                if t not in V_PLANES[j]:
                     nc.scalar.activation(
-                        out=sq_t[r][:, :, t, :],
-                        in_=xs_t[r][:].rearrange("p c (b i) -> p (c b) i", i=8),
+                        out=sq_t[j][:, :, t, :],
+                        in_=x_all[:, 2 * j : 2 * j + 2, :].rearrange("p c (b i) -> p (c b) i", i=8),
                         func=ACT.Square,
                         bias=gneg[:, t : t + 1],
                         scale=1.0,
                     )
 
-        def exp_s(r):
-            bg = work.tile([P, NCOL, 4], BF16, align_bytes=64, name="bg")
-            nc.scalar.activation(
-                out=bg[:].rearrange("p (c i) t -> p c t i", i=8),
-                in_=sq_t[r][:],
-                func=ACT.Exp,
-                scale=-20.0,
-            )
-            bg_t[r] = bg
+        def exp_s(j, pieces):
+            bg = work2.tile([P, NCOL, 4], BF16, align_bytes=64, name="bg")
+            bg_t[N0 + j] = bg
+            n = NCOL // pieces
+            for h in range(pieces):
+                nc.scalar.activation(
+                    out=bg[:, h * n : (h + 1) * n, :].rearrange("p (c i) t -> p c t i", i=8),
+                    in_=sq_t[j][:, h * n // 8 : (h + 1) * n // 8],
+                    func=ACT.Exp,
+                    scale=-20.0,
+                )
+                if pieces > 1:
+                    if h == 0:
+                        b_tiles(N0 + j)
+                    b_quant(N0 + j, h * n, n)
+                    for bt in range(2 * (h % 2), 2 * (h % 2) + 2):
+                        mx(N0 + j, h // 2, bt)
 
         def b_tiles(r):
-            bc = work.tile([P, NCOL], U32, align_bytes=64, name="bc")
-            bs = work.tile([P, NCOL], U8, align_bytes=64, name="bs")
+            bc = work3.tile([P, NCOL], U32, align_bytes=64, name="bc")
+            bs = work3.tile([P, NCOL], U8, align_bytes=64, name="bs")
             bq_t[r] = (bc, bs)
 
         def b_quant(r, lo, n):
@@ -317,25 +300,34 @@ def tile_rbfkanlayer_kernel(tc, x, spline_weight, base_weight, grid, out):
                 in_=bg_t[r][:, lo : lo + n, :].rearrange("p n t -> p (n t)"),
             )
 
-        def z_transpose(r):
+        def whole_round_quant(r):
+            b_tiles(r)
+            b_quant(r, 0, NCOL)
+
+        def whole_round_mx(r):
+            for c in range(2):
+                for bt in range(NBT):
+                    mx(r, c, bt)
+
+        def z_transpose(pi):
             ztp = ps1.tile([P, 2, 512], BF16, tag="ex", name="ztp")
             for c in range(2):
                 for bt in range(NBT):
-                    nc.tensor.transpose(
-                        ztp[:, c, bt * P : (bt + 1) * P], zb[:, bt, 2 * (r - NR) + c, :], ident[:]
-                    )
-            ex_t[r] = ztp
+                    nc.tensor.transpose(ztp[:, c, bt * P : (bt + 1) * P], zb[:, pi, bt, c, :], ident[:])
+            ex_t[100 + pi] = ztp
 
-        def z_copy(r):
-            zt = work.tile([P, 2, 512], BF16, name="zt")
-            nc.scalar.copy(out=zt[:], in_=ex_t[r][:])
-            zt_t[r] = zt
+        def z_copy(pi):
+            zt = work2.tile([P, 2, 512], BF16, name="zt")
+            nc.scalar.copy(out=zt[:], in_=ex_t[100 + pi][:])
+            zt_t[pi] = zt
 
         def arg_pe(v):
-            r = NR + v // 8
             bt = (v % 8) // 2
             c = v % 2
-            if v % 3 == 2:
+            k = v % 4 if v >= 24 else 1 + v % 3
+            if k == 0:
+                arg = ps1.tile([P, 4, P], F32, tag="ex", name="arg")
+            elif k == 1:
                 arg = ps1.tile([P, 4, P], F32, tag="xv", name="arg")
             else:
                 arg = ps2.tile([P, 4, P], F32, tag="xs", name="arg")
@@ -343,110 +335,159 @@ def tile_rbfkanlayer_kernel(tc, x, spline_weight, base_weight, grid, out):
                 nc.tensor.matmul(
                     out=arg[:, t, :],
                     lhsT=lmat[:, t].rearrange("p a b -> p (a b)"),
-                    rhs=zt_t[r][:, c, bt * P : (bt + 1) * P],
+                    rhs=zt_t[v // 8][:, c, bt * P : (bt + 1) * P],
                     start=True,
                     stop=True,
                 )
             arg_t[v] = arg
 
         def arg_exp(v):
-            r = NR + v // 8
             lo = ((v % 8) // 2) * 256 + (v % 2) * P
             nc.scalar.activation(
-                out=bg_t[r][:, lo : lo + P, :],
+                out=bg_t[PR[v // 8]][:, lo : lo + P, :],
                 in_=arg_t[v][:].rearrange("p t n -> p n t"),
                 func=ACT.Exp,
             )
 
+        def finish(bt):
+            res = work2.tile([P, O], F32, name="res")
+            nc.vector.tensor_tensor(out=res[:], in0=acc[bt][:], in1=base_sb[:, bt, :], op=ALU.add)
+            nc.sync.dma_start(out=out[bt * P : (bt + 1) * P, :], in_=res[:])
+
+        def p_block(pi, fill):
+            r = PR[pi]
+            bg_t[r] = work2.tile([P, NCOL, 4], BF16, align_bytes=64, name="bg")
+            for bt in range(NBT):
+                for c in range(2):
+                    v = pi * 8 + bt * 2 + c
+                    arg_exp(v)
+                    if v + 3 < 24:
+                        arg_pe(v + 3)
+                if pi < 2 and bt == 0:
+                    z_transpose(pi + 1)
+                if pi < 2 and bt == 1:
+                    z_copy(pi + 1)
+                for f in fill[bt]:
+                    f()
+                if bt == 0 and r >= 1:
+                    whole_round_quant(r - 1)
+
+        def last_block():
+            r = ROUNDS - 1
+            bg_t[r] = work2.tile([P, NCOL, 4], BF16, align_bytes=64, name="bg")
+            b_tiles(r)
+            for bt in range(NBT):
+                for c in range(2):
+                    v = 24 + bt * 2 + c
+                    arg_exp(v)
+                    if v + 4 < 32:
+                        arg_pe(v + 4)
+                b_quant(r, bt * 256, 256)
+                for c in range(2):
+                    mx(r, c, bt)
+                if bt >= 1:
+                    finish(bt - 1)
+            finish(3)
+
         make_identity(nc, ident[:])
         nc.sync.dma_start(out=gb[:], in_=grid.partition_broadcast(P))
         nc.sync.dma_start(out=x_sb[:], in_=x.rearrange("(t p) i -> p t i", p=P))
-        for r in range(4):
+        for r in range(3):
             w_load(r)
-        nc.sync.dma_start(out=bw_sb[:], in_=base_weight.rearrange("(t p) i -> p t i", p=P))
         warm = const.tile([P, 1], F32)
         nc.vector.memset(warm[:], 0.0)
         warm2 = const.tile([P, 1], F32)
         nc.scalar.activation(out=warm2[:], in_=warm[:], func=ACT.Exp)
-        grid_scalars()
-        x_repeat(0)
-        x_transpose(0)
-        x_repeat(1)
-        exponent_weights()
-        squares_v(0)
+        for pi in range(4):
+            nc.gpsimd.memset(zb[:, pi], 0.0)
+            nc.gpsimd.memset(zb[:, pi, :, :, 16:19], 1.0)
+        nc.vector.memset(alpha[0:32, :], 32.0)
+        nc.vector.memset(alpha[32:64, :], 8.0)
+        nc.vector.memset(alpha[64:128, :], 0.0)
+        nc.vector.memset(beta[0:64, :], 0.0)
+        nc.vector.memset(beta[64:128, :], -20.0)
+        from_identity()
+        base_pe(0)
+        base_pe(1)
+        exponent_weights(z_rows(0, nc.vector))
+        z_transpose(0)
+        z_copy(0)
+        base_v(0)
+        base_v(1)
+        nc.sync.dma_start(out=scratch.rearrange("(t p) b -> p t b", p=P), in_=xT[:])
 
-        for s in range(NR):
-            if s + 1 < NR:
-                x_transpose(s + 1)
-            else:
-                z_transpose(NR)
-            squares_s(s)
-            if 1 <= s <= 8:
-                base_pe(s - 1)
-            if s == NR - 1:
-                z_copy(NR)
-            w_group(s, 0)
-            w_group(s, 1)
-            if s >= 1:
-                b_tiles(s - 1)
-                b_quant(s - 1, 0, NCOL)
-                for c in range(2):
-                    for bt in range(NBT):
-                        mx(s - 1, c, bt, c * 512 + bt * P)
-            if s + 1 < NR:
-                squares_v(s + 1)
-            else:
-                w_group(s + 1, 0)
-                w_group(s + 1, 1)
-            w_quant(s)
-            if 1 <= s <= 8:
-                base_v(s - 1)
-            if s + 2 < NR:
-                x_repeat(s + 2)
-            if s < 7:
-                exponent_rows(s)
-            if s == NR - 1:
-                w_quant(s + 1)
-            exp_s(s)
-            if s + 4 < ROUNDS:
-                w_load(s + 4)
+        def x_back(k):
+            lo, hi = X_CHUNKS[k]
+            for rep in range(8):
+                nc.sync.dma_start(
+                    out=x_all[rep:P:8, lo:hi, :],
+                    in_=scratch.rearrange("(c l) b -> l c b", l=16)[:, 2 * N0 + lo : 2 * N0 + hi, :],
+                )
 
-        NU = 8 * PE_ROUNDS
+        x_back(0)
+        w_load(3)
+        nc.sync.dma_start(out=bw_sb[:], in_=base_weight.rearrange("(t p) i -> p t i", p=P))
+        x_back(1)
+        x_back(2)
         for v in range(3):
             arg_pe(v)
-        for r in range(NR, ROUNDS):
-            last = r == ROUNDS - 1
-            bg_t[r] = work.tile([P, NCOL, 4], BF16, align_bytes=64, name="bg")
-            if not last:
-                z_transpose(r + 1)
-            if r == NR:
-                b_tiles(r - 1)
-                b_quant(r - 1, 0, NCOL)
-                for c in range(2):
-                    for bt in range(NBT):
-                        mx(r - 1, c, bt, c * 512 + bt * P)
-            b_tiles(r)
-            for bt in range(NBT):
-                for c in range(2):
-                    v = (r - NR) * 8 + bt * 2 + c
-                    arg_exp(v)
-                    if v + 3 < NU:
-                        arg_pe(v + 3)
-                if not last and bt == 1:
-                    z_copy(r + 1)
-                if not last and bt < 2:
-                    w_group(r + 1, bt)
-                if not last and bt == 2:
-                    w_quant(r + 1)
-                b_quant(r, bt * 256, 256)
-                for c in range(2):
-                    mx(r, c, bt, bt * 256 + c * P)
-                if last and bt >= 1:
-                    res = small.tile([P, O], F32, name="res")
-                    nc.vector.tensor_tensor(
-                        out=res[:], in0=acc[bt - 1][:], in1=base_sb[:, bt - 1, :], op=ALU.add
-                    )
-                    nc.sync.dma_start(out=out[(bt - 1) * P : bt * P, :], in_=res[:])
-        res = small.tile([P, O], F32, name="res")
-        nc.vector.tensor_tensor(out=res[:], in0=acc[3][:], in1=base_sb[:, 3, :], op=ALU.add)
-        nc.sync.dma_start(out=out[3 * P : 4 * P, :], in_=res[:])
+        for pi in range(1, 4):
+            for f in z_rows(pi, nc.gpsimd):
+                f()
+        w_group(0, 0)
+        w_group(0, 1)
+        grid_scalars()
+        w_quant(0)
+
+        p_block(
+            0,
+            [[], [lambda: w_group(1, 0)], [lambda: w_group(1, 1)], [lambda: w_quant(1)]],
+        )
+        p_block(
+            1,
+            [
+                [lambda: w_group(2, 0)],
+                [lambda: w_group(2, 1)],
+                [lambda: w_quant(2)],
+                [lambda: diff_v(0)],
+            ],
+        )
+        p_block(
+            2,
+            [
+                [lambda: w_group(3, 0), lambda: squares_v(0)],
+                [lambda: w_group(3, 1), lambda: diff_v(1)],
+                [lambda: w_quant(3), lambda: squares_v(1)],
+                [],
+            ],
+        )
+
+        squares_s(0)
+        for j in range(NR):
+            r = N0 + j
+            if j + 1 < NR:
+                squares_s(j + 1)
+            if 1 <= j <= 6:
+                base_pe(j + 1)
+            if j == NR - 1:
+                for v in range(24, 28):
+                    arg_pe(v)
+            if j == 9:
+                z_transpose(3)
+            if j == 10:
+                z_copy(3)
+            w_group(r + 1, 0)
+            if j + 2 < NR:
+                diff_v(j + 2)
+            w_group(r + 1, 1)
+            if j + 2 < NR:
+                squares_v(j + 2)
+            whole_round_quant(r - 1)
+            for rr in MX_PLAN.get(j, (r - 1,)):
+                whole_round_mx(rr)
+            w_quant(r + 1)
+            if 1 <= j <= 6:
+                base_v(j + 1)
+            exp_s(j, 4 if j == NR - 1 else 1)
+
+        last_block()

@@ -254,9 +254,15 @@ def tile_rbfkanlayer_kernel(tc, x, spline_weight, base_weight, grid, out):
                 )
 
         def squares_v(j):
-            planes = V_PLANES[j]
-            dv = sq_t[j][:, :, planes[0] : planes[-1] + 1, :]
-            nc.vector.tensor_tensor(out=dv, in0=dv, in1=dv, op=ALU.mult)
+            for t in V_PLANES[j]:
+                nc.vector.scalar_tensor_tensor(
+                    out=sq_t[j][:, :, t, :],
+                    in0=x_all[:, 2 * j : 2 * j + 2, :].rearrange("p c (b i) -> p (c b) i", i=8),
+                    scalar=gneg[:, t : t + 1],
+                    in1=sq_t[j][:, :, t, :],
+                    op0=ALU.add,
+                    op1=ALU.mult,
+                )
 
         def squares_s(j):
             for t in range(4):

@@ -18,482 +18,404 @@ I = 512
 O = 512
 G = 32
 NBT = B // P
-ROUNDS = 16
-NCOL = 1024
-PR = (0, 1, 2, 15)
-N0 = 3
-NR = 12
+T = 4
+FI = 4
+NPASS = 32
+NCOL = T * B
 
 FLOPS = 2 * B * I * G * O + 2 * B * I * O
 
-V_PLANES = [(2, 3)] + [(3,)] * (NR - 1)
-MX_PLAN = {0: (0, 1), 1: (2, 3)}
-X_CHUNKS = ((0, 4), (4, 12), (12, 24))
+NA = 9
+PAIRS = (NA + 1) // 2
+KINDS = "AAAAAA" + "SVSVSVSA" * 2 + "SVSVSVS" + "SVA"
+MX_LAG = 2
+WB = 8
+XB = 7
+
+
+def pass_order():
+    a, other = 0, NA
+    order = []
+    for kind in KINDS:
+        if kind == "A":
+            order.append(a)
+            a += 1
+        else:
+            order.append(other)
+            other += 1
+    return order
 
 
 def tile_rbfkanlayer_kernel(tc, x, spline_weight, base_weight, grid, out):
     nc = tc.nc
+    order = pass_order()
+    xsteps = [n for n in range(NPASS) if KINDS[n] != "A"]
     with ExitStack() as ctx:
         const = ctx.enter_context(tc.tile_pool(name="const", bufs=1))
-        wraw = ctx.enter_context(tc.tile_pool(name="wraw", bufs=4))
-        work3 = ctx.enter_context(tc.tile_pool(name="work3", bufs=3))
-        work2 = ctx.enter_context(tc.tile_pool(name="work2", bufs=2))
+        pool = ctx.enter_context(tc.tile_pool(name="pool", bufs=1))
         psacc = ctx.enter_context(tc.psum_pool(name="psacc", bufs=1))
-        ps2 = ctx.enter_context(tc.psum_pool(name="ps2", bufs=2))
-        ps1 = ctx.enter_context(tc.psum_pool(name="ps1", bufs=1))
+        psb = ctx.enter_context(tc.psum_pool(name="psb", bufs=1))
         ctx.enter_context(tc.manual_schedule())
 
         ident = const.tile([P, P], BF16)
         gb = const.tile([P, G], BF16)
         x_sb = const.tile([P, NBT, I], BF16)
         bw_sb = const.tile([P, NBT, I], BF16)
-        gneg = const.tile([P, 4], F32)
+        xT = const.tile([P, FI, B], BF16)
+        bwT = const.tile([P, FI, O], BF16)
         base_sb = const.tile([P, NBT, O], F32)
-        xT = const.tile([P, 4, B], BF16)
-        bwT = const.tile([P, 4, O], BF16)
-        zb = const.tile([P, 4, NBT, 2, P], BF16)
-        lmat = const.tile([P, 4, 16, 8], BF16)
-        x_all = const.tile([P, 2 * NR, B], BF16)
+        z = const.tile([P, NBT, PAIRS, P], BF16)
+        q32 = const.tile([P, NBT, PAIRS, G], F32)
+        zt = const.tile([P, PAIRS, B], BF16)
+        lmat = const.tile([P, 32, G], BF16)
+        mask = const.tile([P, G], F32)
+        prod = const.tile([P, G], F32)
+        gsel = const.tile([P, 1], F32)
+        gneg = const.tile([P, 1], F32)
+        g2neg = const.tile([P, 1], F32)
+        gbias = const.tile([P, 1], F32)
+        alpha = const.tile([P, 1], F32)
+        beta = const.tile([P, 1], F32)
+        coef = const.tile([P, G], F32)
+        warm = const.tile([P, 1], F32)
+        warm2 = const.tile([P, 1], F32)
         acc = [psacc.tile([P, O], F32, name="acc%d" % bt) for bt in range(NBT)]
-        scratch = out.bitcast(BF16)[:, 0:B]
+        scratch = out.bitcast(BF16)[0 : B // 2].rearrange("r (h b) -> (r h) b", h=2)
 
         wr_t = {}
         wg_t = {}
         wq_t = {}
+        xr_t = {}
         sq_t = {}
         bg_t = {}
         bq_t = {}
-        zt_t = {}
-        arg_t = {}
-        ex_t = {}
 
-        mask8 = const.tile([P, 8], F32)
-        e3 = const.tile([P, 3], F32)
-        msum = const.tile([P, 16], F32)
-        alpha = const.tile([P, 1], F32)
-        beta = const.tile([P, 1], F32)
-        pc = const.tile([P, G], F32)
-        ag = const.tile([P, G], F32)
+        units = []
+        filled = []
+        used = [0]
 
-        def from_identity():
-            nc.vector.tensor_reduce(
-                out=mask8[:], in_=ident[:].rearrange("p (a q) -> p q a", q=8), axis=AX.X, op=ALU.add
-            )
-            nc.vector.tensor_copy(out=e3[:], in_=ident[:, 16:19])
-            nc.vector.tensor_reduce(
-                out=msum[:],
-                in_=ident[:].rearrange("p (g h i) -> p h i g", g=4, h=2)[:, 0],
-                axis=AX.X,
-                op=ALU.add,
-            )
+        def fill_to(n):
+            while len(filled) < min(n, len(units)) and units[len(filled)][1] <= used[0]:
+                filled.append(units[len(filled)][0](len(filled) % 4))
 
-        def grid_scalars():
-            prod = const.tile([P, 4, 8], F32, name="prod")
-            nc.vector.tensor_tensor(
-                out=prod[:],
-                in0=gb[:].rearrange("p (q t) -> p t q", t=4),
-                in1=mask8[:].unsqueeze(1).to_broadcast([P, 4, 8]),
-                op=ALU.mult,
-            )
-            gsel = const.tile([P, 4], F32, name="gsel")
-            nc.vector.tensor_reduce(out=gsel[:], in_=prod[:], axis=AX.X, op=ALU.add)
-            nc.vector.tensor_scalar(
-                out=gneg[:], in0=gsel[:], scalar1=-1.0, scalar2=None, op0=ALU.mult
-            )
+        def next_unit():
+            t = filled[used[0]]
+            used[0] += 1
+            return t
 
-        def exponent_weights(fill):
-            shape = [P, 4, 16, 8]
-            cc = const.tile([P, G], F32, name="cc")
-            nc.vector.scalar_tensor_tensor(
-                out=cc[:], in0=gb[:], scalar=-20.0, in1=gb[:], op0=ALU.mult, op1=ALU.mult
-            )
-            nc.vector.tensor_scalar(
-                out=ag[:], in0=gb[:], scalar1=alpha[:], scalar2=beta[:], op0=ALU.mult, op1=ALU.add
-            )
-            c1 = const.tile([P, G], BF16, name="c1")
-            nc.vector.tensor_copy(out=c1[:], in_=cc[:])
-            tmp = const.tile(shape, F32, name="tmp")
-            nc.vector.tensor_tensor(
-                out=tmp[:],
-                in0=ag[:].rearrange("p (q t) -> p t q", t=4).unsqueeze(2).to_broadcast(shape),
-                in1=msum[:].unsqueeze(1).unsqueeze(3).to_broadcast(shape),
-                op=ALU.mult,
-            )
-            r1 = const.tile([P, G], F32, name="r1")
-            nc.vector.tensor_tensor(out=r1[:], in0=cc[:], in1=c1[:], op=ALU.subtract)
-            pa = const.tile([P, G], F32, name="pa")
-            nc.vector.tensor_scalar(out=pa[:], in0=c1[:], scalar1=e3[:, 0:1], scalar2=None, op0=ALU.mult)
-            fill[0]()
-            c2 = const.tile([P, G], BF16, name="c2")
-            nc.vector.tensor_copy(out=c2[:], in_=r1[:])
-            fill[1]()
-            fill[2]()
-            c3 = const.tile([P, G], F32, name="c3")
-            nc.vector.tensor_tensor(out=c3[:], in0=r1[:], in1=c2[:], op=ALU.subtract)
-            pb = const.tile([P, G], F32, name="pb")
-            nc.vector.scalar_tensor_tensor(
-                out=pb[:], in0=c2[:], scalar=e3[:, 1:2], in1=pa[:], op0=ALU.mult, op1=ALU.add
-            )
-            fill[3]()
-            fill[4]()
-            nc.vector.scalar_tensor_tensor(
-                out=pc[:], in0=c3[:], scalar=e3[:, 2:3], in1=pb[:], op0=ALU.mult, op1=ALU.add
-            )
-            nc.vector.tensor_tensor(
-                out=lmat[:],
-                in0=tmp[:],
-                in1=pc[:].rearrange("p (q t) -> p t q", t=4).unsqueeze(2).to_broadcast(shape),
-                op=ALU.add,
-            )
+        def refill():
+            fill_to(used[0] + 4)
 
-        def z_rows(pi, eng):
-            f0 = 32 * PR[pi]
-            xp = x_sb[:, :, f0 : f0 + 32].rearrange("p t (c i) -> p t c i", i=16)
-            q32 = work2.tile([P, NBT, 2, 16], F32, name="q32")
-            z = zb[:, pi]
-            return [
-                lambda: eng.tensor_tensor(out=q32[:], in0=xp, in1=xp, op=ALU.mult),
-                lambda: eng.tensor_copy(out=z[:, :, :, 0:16], in_=xp),
-                lambda: eng.tensor_copy(out=z[:, :, :, 64:80], in_=q32[:]),
-                lambda: eng.tensor_copy(out=z[:, :, :, 32:48], in_=xp),
-                lambda: eng.tensor_tensor(
-                    out=z[:, :, :, 96:112], in0=q32[:], in1=z[:, :, :, 64:80], op=ALU.subtract
-                ),
-            ]
+        def bank(k, shape, dtype):
+            return psb.tile(shape, dtype, tag="b%d" % k, name="bk")
 
-        def base_pe(j):
-            if j < 4:
-                src = (x_sb, bw_sb)[j // 2]
-                h = j % 2
-                if j < 2:
-                    tp = ps2.tile([P, 2, 512], BF16, tag="xs", name="tp")
-                else:
-                    tp = ps1.tile([P, 2, 512], BF16, tag="ex", name="tp")
-                for k in range(2):
+        def fill_xT(h):
+            def f(k):
+                tp = bank(k, [P, 2, 512], BF16)
+                for j in range(2):
                     for bt in range(NBT):
                         nc.tensor.transpose(
-                            tp[:, k, bt * P : (bt + 1) * P],
-                            src[:, bt, (2 * h + k) * P : (2 * h + k + 1) * P],
-                            ident[:],
+                            tp[:, j, bt * P : (bt + 1) * P], x_sb[:, bt, 2 * h + j : I : FI], ident[:]
                         )
-                ex_t[j] = tp
-            else:
-                bt = j - 4
-                bp = ps1.tile([P, O], F32, tag="ex", name="bp")
-                for it in range(4):
+                return tp
+
+            return f
+
+        def fill_bwT(h):
+            def f(k):
+                tp = bank(k, [P, 2, 512], BF16)
+                for j in range(2):
+                    for bt in range(NBT):
+                        nc.tensor.transpose(
+                            tp[:, j, bt * P : (bt + 1) * P], bw_sb[:, bt, 2 * h + j : I : FI], ident[:]
+                        )
+                return tp
+
+            return f
+
+        def fill_base(bt):
+            def f(k):
+                tp = bank(k, [P, O], F32)
+                for j in range(FI):
                     nc.tensor.matmul(
-                        out=bp[:],
-                        lhsT=xT[:, it, bt * P : (bt + 1) * P],
-                        rhs=bwT[:, it, :],
-                        start=(it == 0),
-                        stop=(it == 3),
+                        out=tp[:],
+                        lhsT=xT[:, j, bt * P : (bt + 1) * P],
+                        rhs=bwT[:, j, :],
+                        start=(j == 0),
+                        stop=(j == FI - 1),
                     )
-                ex_t[j] = bp
+                return tp
 
-        def base_v(j):
-            if j < 4:
-                dst = (xT, bwT)[j // 2]
-                h = j % 2
-                nc.vector.tensor_copy(out=dst[:, 2 * h : 2 * h + 2, :], in_=ex_t[j][:])
-            else:
-                nc.vector.tensor_copy(out=base_sb[:, j - 4, :], in_=ex_t[j][:])
+            return f
 
-        def w_load(r):
-            wr = wraw.tile([P, 2, 4, O], BF16, name="wr")
+        def fill_z(prs):
+            def f(k):
+                tp = bank(k, [P, len(prs), 512], BF16)
+                for j, pr in enumerate(prs):
+                    for bt in range(NBT):
+                        nc.tensor.transpose(tp[:, j, bt * P : (bt + 1) * P], z[:, bt, pr, :], ident[:])
+                return tp
+
+            return f
+
+        def fill_arg(c, bt):
+            def f(k):
+                tp = bank(k, [P, T, P], F32)
+                for t in range(T):
+                    m0 = 16 * (c % 2) + 4 * t
+                    nc.tensor.matmul(
+                        out=tp[:, t, :],
+                        lhsT=lmat[:, m0 : m0 + 4, :].rearrange("p f g -> p (f g)"),
+                        rhs=zt[:, c // 2, bt * P : (bt + 1) * P],
+                        start=True,
+                        stop=True,
+                    )
+                return tp
+
+            return f
+
+        def w_load(n):
+            c = order[n]
+            wr = pool.tile([P, T, O], BF16, name="wr", bufs=WB)
             nc.sync.dma_start(
                 out=wr[:],
-                in_=spline_weight[r * 1024 : (r + 1) * 1024, :].rearrange(
-                    "(c p j) o -> p c j o", c=2, p=P, j=4
-                ),
+                in_=spline_weight[c * 512 : (c + 1) * 512, :].rearrange("(t p) o -> p t o", t=T),
             )
-            wr_t[r] = wr
+            wr_t[n] = wr
 
-        def w_group(r, c):
-            if c == 0:
-                wg_t[r] = work2.tile([P, 2, O, 4], BF16, align_bytes=64, name="wg")
+        def w_group(n):
+            wg = pool.tile([P, O, T], BF16, align_bytes=64, name="wg", bufs=3)
             nc.vector.tensor_copy(
-                out=wg_t[r][:, c].rearrange("p (c i) t -> p c t i", i=4),
-                in_=wr_t[r][:, c].rearrange("p t (c i) -> p c t i", i=4),
+                out=wg[:].rearrange("p (c i) t -> p c t i", i=4),
+                in_=wr_t[n][:].rearrange("p t (c i) -> p c t i", i=4),
             )
-            if c == 1 and r + 4 < ROUNDS:
-                w_load(r + 4)
+            wg_t[n] = wg
+            if n + WB < NPASS:
+                w_load(n + WB)
 
-        def w_quant(r):
-            wc = work3.tile([P, NCOL], U32, align_bytes=64, name="wc", bufs=4)
-            ws = work3.tile([P, NCOL], U8, align_bytes=64, name="ws", bufs=4)
+        def w_quant(n):
+            wc = pool.tile([P, O], U32, align_bytes=64, name="wc", bufs=8)
+            ws = pool.tile([P, O], U8, align_bytes=64, name="ws", bufs=8)
             nc.vector.quantize_mx(
-                out=wc[:].bitcast(FP8X4),
-                scales=ws[:],
-                in_=wg_t[r][:].rearrange("p c o t -> p (c o t)"),
+                out=wc[:].bitcast(FP8X4), scales=ws[:], in_=wg_t[n][:].rearrange("p o t -> p (o t)")
             )
-            wq_t[r] = (wc, ws)
+            wq_t[n] = (wc, ws)
 
-        def mx(r, c, bt):
-            lo = bt * 256 + c * P if r in PR else c * 512 + bt * P
-            bc, bs = bq_t[r]
-            wc, ws = wq_t[r]
+        def squares(n):
+            sq_t[n] = pool.tile([P, B // 4, T, 4], F32, name="sq", bufs=4)
+            sv = sq_t[n][:].rearrange("p c t i -> p t c i")
+            xv = xr_t[n][:].rearrange("p (t c i) -> p t c i", t=T, i=4)
+            if KINDS[n] == "V":
+                for t in range(T):
+                    nc.vector.scalar_tensor_tensor(
+                        out=sv[:, t], in0=xv[:, t], scalar=g2neg[:], in1=xv[:, t], op0=ALU.add, op1=ALU.mult
+                    )
+            else:
+                nc.scalar.activation(out=sv, in_=xv, func=ACT.Square, bias=gneg[:], scale=1.0)
+            j = xsteps.index(n) + XB
+            if j < len(xsteps):
+                x_load(xsteps[j])
+
+        def new_bg(n):
+            bg_t[n] = pool.tile([P, B, T], BF16, align_bytes=64, name="bg", bufs=4)
+            return bg_t[n]
+
+        def exp_sq(n):
+            bg = new_bg(n)
+            nc.scalar.activation(
+                out=bg[:].rearrange("p (c i) t -> p c t i", i=4),
+                in_=sq_t[n][:],
+                func=ACT.Exp,
+                bias=gbias[:] if KINDS[n] == "V" else 0.0,
+                scale=-20.0,
+            )
+
+        def exp_a_piece(n, bt):
+            tp = next_unit()
+            nc.scalar.activation(
+                out=bg_t[n][:, bt * P : (bt + 1) * P, :],
+                in_=tp[:].rearrange("p t b -> p b t"),
+                func=ACT.Exp,
+                bias=gbias[:],
+                scale=20.0,
+            )
+            refill()
+
+        def b_tiles(n):
+            bc = pool.tile([P, B], U32, align_bytes=64, name="bc", bufs=5)
+            bs = pool.tile([P, B], U8, align_bytes=64, name="bs", bufs=5)
+            bq_t[n] = (bc, bs)
+
+        def b_quant(n, lo, cols):
+            bc, bs = bq_t[n]
+            nc.vector.quantize_mx(
+                out=bc[:, lo : lo + cols].bitcast(FP8X4),
+                scales=bs[:, lo : lo + cols],
+                in_=bg_t[n][:, lo : lo + cols, :].rearrange("p b t -> p (b t)"),
+            )
+
+        def mx(n, bt):
+            bc, bs = bq_t[n]
+            wc, ws = wq_t[n]
             nc.tensor.matmul_mx(
                 out=acc[bt][:],
-                lhsT=bc[:, lo : lo + P].bitcast(FP8X4),
-                lhsT_scale=bs[:, lo : lo + P],
-                rhs=wc[:, c * 512 : (c + 1) * 512].bitcast(FP8X4),
-                rhs_scale=ws[:, c * 512 : (c + 1) * 512],
-                start=(r == 0 and c == 0),
-                stop=(r == ROUNDS - 1 and c == 1),
+                lhsT=bc[:, bt * P : (bt + 1) * P].bitcast(FP8X4),
+                lhsT_scale=bs[:, bt * P : (bt + 1) * P],
+                rhs=wc[:].bitcast(FP8X4),
+                rhs_scale=ws[:],
+                start=(n == 0),
+                stop=(n == NPASS - 1),
             )
 
-        def diff_v(j):
-            sq_t[j] = work3.tile([P, NCOL // 8, 4, 8], F32, name="sq")
-            for t in V_PLANES[j]:
-                nc.vector.tensor_scalar(
-                    out=sq_t[j][:, :, t, :],
-                    in0=x_all[:, 2 * j : 2 * j + 2, :].rearrange("p c (b i) -> p (c b) i", i=8),
-                    scalar1=gneg[:, t : t + 1],
-                    scalar2=None,
-                    op0=ALU.add,
+        def x_load(n):
+            c = order[n]
+            xr = pool.tile([P, NCOL], BF16, name="xr", bufs=XB)
+            for f in (0, 2, 1, 3):
+                r0 = f * P + 4 * c
+                nc.sync.dma_start(
+                    out=xr[32 * f : 32 * f + 32, :],
+                    in_=scratch[r0 : r0 + 4, :].rearrange("r b -> (r b)").partition_broadcast(32),
                 )
-
-        def squares_v(j):
-            for t in V_PLANES[j]:
-                nc.vector.scalar_tensor_tensor(
-                    out=sq_t[j][:, :, t, :],
-                    in0=x_all[:, 2 * j : 2 * j + 2, :].rearrange("p c (b i) -> p (c b) i", i=8),
-                    scalar=gneg[:, t : t + 1],
-                    in1=sq_t[j][:, :, t, :],
-                    op0=ALU.add,
-                    op1=ALU.mult,
-                )
-
-        def squares_s(j):
-            for t in range(4):
-                if t not in V_PLANES[j]:
-                    nc.scalar.activation(
-                        out=sq_t[j][:, :, t, :],
-                        in_=x_all[:, 2 * j : 2 * j + 2, :].rearrange("p c (b i) -> p (c b) i", i=8),
-                        func=ACT.Square,
-                        bias=gneg[:, t : t + 1],
-                        scale=1.0,
-                    )
-
-        def exp_s(j, pieces):
-            bg = work2.tile([P, NCOL, 4], BF16, align_bytes=64, name="bg")
-            bg_t[N0 + j] = bg
-            n = NCOL // pieces
-            for h in range(pieces):
-                nc.scalar.activation(
-                    out=bg[:, h * n : (h + 1) * n, :].rearrange("p (c i) t -> p c t i", i=8),
-                    in_=sq_t[j][:, h * n // 8 : (h + 1) * n // 8],
-                    func=ACT.Exp,
-                    scale=-20.0,
-                )
-                if pieces > 1:
-                    if h == 0:
-                        b_tiles(N0 + j)
-                    b_quant(N0 + j, h * n, n)
-                    for bt in range(2 * (h % 2), 2 * (h % 2) + 2):
-                        mx(N0 + j, h // 2, bt)
-
-        def b_tiles(r):
-            bc = work3.tile([P, NCOL], U32, align_bytes=64, name="bc")
-            bs = work3.tile([P, NCOL], U8, align_bytes=64, name="bs")
-            bq_t[r] = (bc, bs)
-
-        def b_quant(r, lo, n):
-            bc, bs = bq_t[r]
-            nc.vector.quantize_mx(
-                out=bc[:, lo : lo + n].bitcast(FP8X4),
-                scales=bs[:, lo : lo + n],
-                in_=bg_t[r][:, lo : lo + n, :].rearrange("p n t -> p (n t)"),
-            )
-
-        def whole_round_quant(r):
-            b_tiles(r)
-            b_quant(r, 0, NCOL)
-
-        def whole_round_mx(r):
-            for c in range(2):
-                for bt in range(NBT):
-                    mx(r, c, bt)
-
-        def z_transpose(pi):
-            ztp = ps1.tile([P, 2, 512], BF16, tag="ex", name="ztp")
-            for c in range(2):
-                for bt in range(NBT):
-                    nc.tensor.transpose(ztp[:, c, bt * P : (bt + 1) * P], zb[:, pi, bt, c, :], ident[:])
-            ex_t[100 + pi] = ztp
-
-        def z_copy(pi):
-            zt = work2.tile([P, 2, 512], BF16, name="zt")
-            nc.scalar.copy(out=zt[:], in_=ex_t[100 + pi][:])
-            zt_t[pi] = zt
-
-        def arg_pe(v):
-            bt = (v % 8) // 2
-            c = v % 2
-            k = v % 4 if v >= 24 else 1 + v % 3
-            if k == 0:
-                arg = ps1.tile([P, 4, P], F32, tag="ex", name="arg")
-            elif k == 1:
-                arg = ps1.tile([P, 4, P], F32, tag="xv", name="arg")
-            else:
-                arg = ps2.tile([P, 4, P], F32, tag="xs", name="arg")
-            for t in range(4):
-                nc.tensor.matmul(
-                    out=arg[:, t, :],
-                    lhsT=lmat[:, t].rearrange("p a b -> p (a b)"),
-                    rhs=zt_t[v // 8][:, c, bt * P : (bt + 1) * P],
-                    start=True,
-                    stop=True,
-                )
-            arg_t[v] = arg
-
-        def arg_exp(v):
-            lo = ((v % 8) // 2) * 256 + (v % 2) * P
-            nc.scalar.activation(
-                out=bg_t[PR[v // 8]][:, lo : lo + P, :],
-                in_=arg_t[v][:].rearrange("p t n -> p n t"),
-                func=ACT.Exp,
-            )
+            xr_t[n] = xr
 
         def finish(bt):
-            res = work2.tile([P, O], F32, name="res")
+            res = pool.tile([P, O], F32, name="res", bufs=2)
             nc.vector.tensor_tensor(out=res[:], in0=acc[bt][:], in1=base_sb[:, bt, :], op=ALU.add)
             nc.sync.dma_start(out=out[bt * P : (bt + 1) * P, :], in_=res[:])
 
-        def p_block(pi, fill):
-            r = PR[pi]
-            bg_t[r] = work2.tile([P, NCOL, 4], BF16, align_bytes=64, name="bg")
-            for bt in range(NBT):
-                for c in range(2):
-                    v = pi * 8 + bt * 2 + c
-                    arg_exp(v)
-                    if v + 3 < 24:
-                        arg_pe(v + 3)
-                if pi < 2 and bt == 0:
-                    z_transpose(pi + 1)
-                if pi < 2 and bt == 1:
-                    z_copy(pi + 1)
-                for f in fill[bt]:
-                    f()
-                if bt == 0 and r >= 1:
-                    whole_round_quant(r - 1)
+        units.append((fill_z([0]), 0))
+        units.append((fill_xT(0), 0))
+        units.append((fill_xT(1), 0))
+        units.append((fill_z([1, 2]), 0))
+        zneed = {0: 1, 1: 4, 2: 4}
+        side = {
+            6: [fill_z([3, 4])],
+            7: [fill_bwT(0)],
+            8: [fill_bwT(1)],
+            10: [fill_base(0)],
+            12: [fill_base(1)],
+            14: [fill_base(2)],
+            16: [fill_base(3)],
+        }
+        for n in range(NPASS):
+            for f in side.get(n, []):
+                units.append((f, zneed["bw"] if n >= 10 else 0))
+                if n == 6:
+                    zneed[3] = zneed[4] = len(units)
+                elif n == 8:
+                    zneed["bw"] = len(units)
+            if KINDS[n] == "A":
+                for bt in range(NBT):
+                    units.append((fill_arg(order[n], bt), zneed[order[n] // 2]))
 
-        def last_block():
-            r = ROUNDS - 1
-            bg_t[r] = work2.tile([P, NCOL, 4], BF16, align_bytes=64, name="bg")
-            b_tiles(r)
-            for bt in range(NBT):
-                for c in range(2):
-                    v = 24 + bt * 2 + c
-                    arg_exp(v)
-                    if v + 4 < 32:
-                        arg_pe(v + 4)
-                b_quant(r, bt * 256, 256)
-                for c in range(2):
-                    mx(r, c, bt)
-                if bt >= 1:
-                    finish(bt - 1)
-            finish(3)
+        def side_copy(n):
+            if n not in side:
+                return
+            tp = next_unit()
+            if n == 6:
+                nc.scalar.copy(out=zt[:, 3:5, :], in_=tp[:])
+            elif n in (7, 8):
+                nc.vector.tensor_copy(out=bwT[:, 2 * (n - 7) : 2 * (n - 7) + 2, :], in_=tp[:])
+            else:
+                nc.vector.tensor_copy(out=base_sb[:, (n - 10) // 2, :], in_=tp[:])
+            refill()
 
         make_identity(nc, ident[:])
         nc.sync.dma_start(out=gb[:], in_=grid.partition_broadcast(P))
         nc.sync.dma_start(out=x_sb[:], in_=x.rearrange("(t p) i -> p t i", p=P))
-        for r in range(3):
-            w_load(r)
-        warm = const.tile([P, 1], F32)
+        for n in range(4):
+            w_load(n)
         nc.vector.memset(warm[:], 0.0)
-        warm2 = const.tile([P, 1], F32)
         nc.scalar.activation(out=warm2[:], in_=warm[:], func=ACT.Exp)
-        for pi in range(4):
-            nc.gpsimd.memset(zb[:, pi], 0.0)
-            nc.gpsimd.memset(zb[:, pi, :, :, 16:19], 1.0)
-        nc.vector.memset(alpha[0:32, :], 32.0)
-        nc.vector.memset(alpha[32:64, :], 8.0)
+        nc.gpsimd.memset(z[:, :, :, 96:128], 0.0)
+        nc.vector.memset(alpha[0:32, :], 2.0)
+        nc.vector.memset(alpha[32:64, :], 0.0)
         nc.vector.memset(alpha[64:128, :], 0.0)
-        nc.vector.memset(beta[0:64, :], 0.0)
-        nc.vector.memset(beta[64:128, :], -20.0)
-        from_identity()
-        base_pe(0)
-        base_pe(1)
-        exponent_weights(z_rows(0, nc.vector))
-        z_transpose(0)
-        z_copy(0)
-        base_v(0)
-        base_v(1)
-        nc.sync.dma_start(out=scratch.rearrange("(t p) b -> p t b", p=P), in_=xT[:])
-
-        def x_back(k):
-            lo, hi = X_CHUNKS[k]
-            for rep in range(8):
-                nc.sync.dma_start(
-                    out=x_all[rep:P:8, lo:hi, :],
-                    in_=scratch.rearrange("(c l) b -> l c b", l=16)[:, 2 * N0 + lo : 2 * N0 + hi, :],
-                )
-
-        x_back(0)
-        w_load(3)
+        nc.vector.memset(beta[0:32, :], 0.0)
+        nc.vector.memset(beta[32:64, :], -1.0)
+        nc.vector.memset(beta[64:96, :], -1.0)
+        nc.vector.memset(beta[96:128, :], 0.0)
+        nc.vector.tensor_reduce(
+            out=mask[:], in_=ident[:].rearrange("p (a q) -> p q a", q=G), axis=AX.X, op=ALU.add
+        )
+        nc.vector.tensor_tensor(out=prod[:], in0=gb[:], in1=mask[:], op=ALU.mult)
+        nc.vector.tensor_scalar(
+            out=coef[:], in0=gb[:], scalar1=alpha[:], scalar2=beta[:], op0=ALU.mult, op1=ALU.add
+        )
+        nc.vector.tensor_reduce(out=gsel[:], in_=prod[:], axis=AX.X, op=ALU.add)
+        nc.vector.tensor_scalar(out=gneg[:], in0=gsel[:], scalar1=-1.0, scalar2=None, op0=ALU.mult)
+        nc.vector.tensor_scalar(out=g2neg[:], in0=gsel[:], scalar1=-2.0, scalar2=None, op0=ALU.mult)
+        nc.vector.scalar_tensor_tensor(
+            out=gbias[:], in0=gsel[:], scalar=-20.0, in1=gsel[:], op0=ALU.mult, op1=ALU.mult
+        )
+        nc.vector.tensor_tensor(
+            out=lmat[:],
+            in0=mask[:].unsqueeze(2).to_broadcast([P, 32, G]),
+            in1=coef[:].unsqueeze(1).to_broadcast([P, 32, G]),
+            op=ALU.mult,
+        )
+        zx = x_sb[:, :, 0 : 32 * PAIRS].rearrange("p t (r i) -> p t r i", i=32)
+        nc.vector.tensor_tensor(out=q32[:], in0=zx, in1=zx, op=ALU.mult)
+        nc.vector.tensor_copy(out=z[:, :, :, 0:32], in_=zx)
+        nc.vector.tensor_copy(out=z[:, :, :, 32:64], in_=q32[:])
+        nc.vector.tensor_tensor(
+            out=z[:, :, :, 64:96], in0=q32[:], in1=z[:, :, :, 32:64], op=ALU.subtract
+        )
+        fill_to(4)
+        tp = next_unit()
+        nc.scalar.copy(out=zt[:, 0:1, :], in_=tp[:])
+        refill()
+        for h in range(2):
+            tp = next_unit()
+            nc.vector.tensor_copy(out=xT[:, 2 * h : 2 * h + 2, :], in_=tp[:])
+            refill()
+        nc.sync.dma_start(out=scratch.rearrange("(f j) b -> j f b", f=FI), in_=xT[:])
+        for k in range(4):
+            x_load(xsteps[k])
+            w_load(4 + k)
         nc.sync.dma_start(out=bw_sb[:], in_=base_weight.rearrange("(t p) i -> p t i", p=P))
-        x_back(1)
-        x_back(2)
-        for v in range(3):
-            arg_pe(v)
-        for pi in range(1, 4):
-            for f in z_rows(pi, nc.gpsimd):
-                f()
-        w_group(0, 0)
-        w_group(0, 1)
-        grid_scalars()
+        for k in range(4, XB):
+            x_load(xsteps[k])
+        tp = next_unit()
+        nc.scalar.copy(out=zt[:, 1:3, :], in_=tp[:])
+        refill()
+        w_group(0)
+        w_group(1)
         w_quant(0)
+        w_quant(1)
 
-        p_block(
-            0,
-            [[], [lambda: w_group(1, 0)], [lambda: w_group(1, 1)], [lambda: w_quant(1)]],
-        )
-        p_block(
-            1,
-            [
-                [lambda: w_group(2, 0)],
-                [lambda: w_group(2, 1)],
-                [lambda: w_quant(2)],
-                [lambda: diff_v(0)],
-            ],
-        )
-        p_block(
-            2,
-            [
-                [lambda: w_group(3, 0), lambda: squares_v(0)],
-                [lambda: w_group(3, 1), lambda: diff_v(1)],
-                [lambda: w_quant(3), lambda: squares_v(1)],
-                [],
-            ],
-        )
-
-        squares_s(0)
-        for j in range(NR):
-            r = N0 + j
-            if j + 1 < NR:
-                squares_s(j + 1)
-            if 1 <= j <= 6:
-                base_pe(j + 1)
-            if j == NR - 1:
-                for v in range(24, 28):
-                    arg_pe(v)
-            if j == 9:
-                z_transpose(3)
-            if j == 10:
-                z_copy(3)
-            w_group(r + 1, 0)
-            if j + 2 < NR:
-                diff_v(j + 2)
-            w_group(r + 1, 1)
-            if j + 2 < NR:
-                squares_v(j + 2)
-            whole_round_quant(r - 1)
-            for rr in MX_PLAN.get(j, (r - 1,)):
-                whole_round_mx(rr)
-            w_quant(r + 1)
-            if 1 <= j <= 6:
-                base_v(j + 1)
-            exp_s(j, 4 if j == NR - 1 else 1)
-
-        last_block()
+        for n in range(NPASS):
+            last = n == NPASS - 1
+            if n + 2 < NPASS:
+                w_group(n + 2)
+            if n >= 1:
+                b_tiles(n - 1)
+                b_quant(n - 1, 0, B)
+            if n + 2 < NPASS:
+                w_quant(n + 2)
+                if KINDS[n + 2] == "V":
+                    squares(n + 2)
+            if n + 1 < NPASS and KINDS[n + 1] == "S":
+                squares(n + 1)
+            side_copy(n)
+            if KINDS[n] != "A":
+                exp_sq(n)
+            else:
+                new_bg(n)
+                if last:
+                    b_tiles(n)
+                    for m in range(n - MX_LAG, n):
+                        for bt in range(NBT):
+                            mx(m, bt)
+                for bt in range(NBT):
+                    exp_a_piece(n, bt)
+                    if last:
+                        b_quant(n, bt * P, P)
+                        mx(n, bt)
+                        if bt >= 1:
+                            finish(bt - 1)
+                if last:
+                    finish(NBT - 1)
+            if n >= MX_LAG and not last:
+                for bt in range(NBT):
+                    mx(n - MX_LAG, bt)

@@ -27,29 +27,26 @@ FLOPS = 2 * B * I * G * O + 2 * B * I * O
 
 NA = 9
 PAIRS = (NA + 1) // 2
-KINDS = "AAAAAA" + "SVSVSVSA" * 2 + "SVSVSVS" + "SVA"
+KINDS = "AAAAAA" + "RVSRVSA" * 2 + "RVS" * 3 + "SVA"
+NREP = KINDS.count("R")
+REP_AHEAD = 4
 MX_LAG = 2
 WB = 8
 XB = 7
 
 
 def pass_order():
-    a, other = 0, NA
+    first = {"A": 0, "R": NA, "V": NA + NREP, "S": NA + NREP + KINDS.count("V")}
     order = []
-    for kind in KINDS:
-        if kind == "A":
-            order.append(a)
-            a += 1
-        else:
-            order.append(other)
-            other += 1
+    for n, kind in enumerate(KINDS):
+        order.append(first[kind] + KINDS[:n].count(kind))
     return order
 
 
 def tile_rbfkanlayer_kernel(tc, x, spline_weight, base_weight, grid, out):
     nc = tc.nc
     order = pass_order()
-    xsteps = [n for n in range(NPASS) if KINDS[n] != "A"]
+    xsteps = [n for n in range(NPASS) if KINDS[n] in "SV"]
     with ExitStack() as ctx:
         const = ctx.enter_context(tc.tile_pool(name="const", bufs=1))
         pool = ctx.enter_context(tc.tile_pool(name="pool", bufs=1))
@@ -64,10 +61,14 @@ def tile_rbfkanlayer_kernel(tc, x, spline_weight, base_weight, grid, out):
         xT = const.tile([P, FI, B], BF16)
         bwT = const.tile([P, FI, O], BF16)
         base_sb = const.tile([P, NBT, O], F32)
-        z = const.tile([P, NBT, PAIRS, P], BF16)
-        q32 = const.tile([P, NBT, PAIRS, G], F32)
+        x0_sb = const.tile([P, NBT, 32], BF16)
+        z0 = const.tile([P, NBT, 1, P], BF16)
+        zr = const.tile([P, NBT, PAIRS - 1, P], BF16)
+        q0 = const.tile([P, NBT, 1, 32], F32)
+        qr = const.tile([P, NBT, PAIRS - 1, 32], F32)
         zt = const.tile([P, PAIRS, B], BF16)
         lmat = const.tile([P, 32, G], BF16)
+        xx = const.tile([P, NBT, 16 * NREP, 2], BF16)
         mask = const.tile([P, G], F32)
         prod = const.tile([P, G], F32)
         gsel = const.tile([P, 1], F32)
@@ -86,6 +87,7 @@ def tile_rbfkanlayer_kernel(tc, x, spline_weight, base_weight, grid, out):
         wg_t = {}
         wq_t = {}
         xr_t = {}
+        xb_t = {}
         sq_t = {}
         bg_t = {}
         bq_t = {}
@@ -93,9 +95,14 @@ def tile_rbfkanlayer_kernel(tc, x, spline_weight, base_weight, grid, out):
         units = []
         filled = []
         used = [0]
+        ready = {-1}
 
         def fill_to(n):
-            while len(filled) < min(n, len(units)) and units[len(filled)][1] <= used[0]:
+            while (
+                len(filled) < min(n, len(units))
+                and units[len(filled)][1] <= used[0]
+                and units[len(filled)][2] in ready
+            ):
                 filled.append(units[len(filled)][0](len(filled) % 4))
 
         def next_unit():
@@ -153,7 +160,22 @@ def tile_rbfkanlayer_kernel(tc, x, spline_weight, base_weight, grid, out):
                 tp = bank(k, [P, len(prs), 512], BF16)
                 for j, pr in enumerate(prs):
                     for bt in range(NBT):
-                        nc.tensor.transpose(tp[:, j, bt * P : (bt + 1) * P], z[:, bt, pr, :], ident[:])
+                        src = z0[:, bt, 0, :] if pr == 0 else zr[:, bt, pr - 1, :]
+                        nc.tensor.transpose(tp[:, j, bt * P : (bt + 1) * P], src, ident[:])
+                return tp
+
+            return f
+
+        def fill_rep(n, h):
+            def f(k):
+                tp = bank(k, [P, T, 256], BF16)
+                for t in range(T):
+                    for j in range(2):
+                        nc.tensor.transpose(
+                            tp[:, t, j * P : (j + 1) * P],
+                            xb_t[n][:, 2 * h + j, 4 * t : 4 * t + 4, :].rearrange("p f g -> p (f g)"),
+                            ident[:],
+                        )
                 return tp
 
             return f
@@ -216,6 +238,32 @@ def tile_rbfkanlayer_kernel(tc, x, spline_weight, base_weight, grid, out):
             if j < len(xsteps):
                 x_load(xsteps[j])
 
+        def repeat_x(n):
+            xb = pool.tile([P, NBT, 16, G], BF16, name="xb", bufs=3)
+            j = order[n] - NA
+            nc.vector.tensor_copy(
+                out=xb[:].rearrange("p t i g -> p (t i g)").bitcast(F32).rearrange("p (t i w) -> p t i w", t=NBT, i=16),
+                in_=xx[:].rearrange("p t i e -> p (t i e)").bitcast(F32).rearrange("p (t i) -> p t i", t=NBT)[
+                    :, :, 16 * j : 16 * j + 16
+                ].unsqueeze(3).to_broadcast([P, NBT, 16, G // 2]),
+            )
+            xb_t[n] = xb
+            ready.add(n)
+            refill()
+
+        def squares_r(n):
+            sq_t[n] = pool.tile([P, B, T], F32, name="sq", bufs=4)
+            for h in range(2):
+                tp = next_unit()
+                nc.scalar.activation(
+                    out=sq_t[n][:, 256 * h : 256 * h + 256, :],
+                    in_=tp[:].rearrange("p t b -> p b t"),
+                    func=ACT.Square,
+                    bias=gneg[:],
+                    scale=1.0,
+                )
+                refill()
+
         def new_bg(n):
             bg_t[n] = pool.tile([P, B, T], BF16, align_bytes=64, name="bg", bufs=4)
             return bg_t[n]
@@ -223,7 +271,7 @@ def tile_rbfkanlayer_kernel(tc, x, spline_weight, base_weight, grid, out):
         def exp_sq(n):
             bg = new_bg(n)
             nc.scalar.activation(
-                out=bg[:].rearrange("p (c i) t -> p c t i", i=4),
+                out=bg[:] if KINDS[n] == "R" else bg[:].rearrange("p (c i) t -> p c t i", i=4),
                 in_=sq_t[n][:],
                 func=ACT.Exp,
                 bias=gbias[:] if KINDS[n] == "V" else 0.0,
@@ -278,18 +326,23 @@ def tile_rbfkanlayer_kernel(tc, x, spline_weight, base_weight, grid, out):
                 )
             xr_t[n] = xr
 
+        def pass_exps(n):
+            if KINDS[n] != "A":
+                exp_sq(n)
+            else:
+                new_bg(n)
+                for bt in range(NBT):
+                    exp_a_piece(n, bt)
+
         def finish(bt):
-            res = pool.tile([P, O], F32, name="res", bufs=2)
+            res = pool.tile([P, O], F32, name="res", bufs=4)
             nc.vector.tensor_tensor(out=res[:], in0=acc[bt][:], in1=base_sb[:, bt, :], op=ALU.add)
             nc.sync.dma_start(out=out[bt * P : (bt + 1) * P, :], in_=res[:])
 
-        units.append((fill_z([0]), 0))
-        units.append((fill_xT(0), 0))
-        units.append((fill_xT(1), 0))
-        units.append((fill_z([1, 2]), 0))
-        zneed = {0: 1, 1: 4, 2: 4}
+        units.append((fill_z([0]), 0, -1))
+        zneed = {0: 1}
         side = {
-            6: [fill_z([3, 4])],
+            0: [fill_xT(0), fill_xT(1), fill_z([1, 2]), fill_z([3, 4])],
             7: [fill_bwT(0)],
             8: [fill_bwT(1)],
             10: [fill_base(0)],
@@ -298,36 +351,50 @@ def tile_rbfkanlayer_kernel(tc, x, spline_weight, base_weight, grid, out):
             16: [fill_base(3)],
         }
         for n in range(NPASS):
-            for f in side.get(n, []):
-                units.append((f, zneed["bw"] if n >= 10 else 0))
-                if n == 6:
-                    zneed[3] = zneed[4] = len(units)
-                elif n == 8:
-                    zneed["bw"] = len(units)
+            if n + 1 < NPASS and KINDS[n + 1] == "R":
+                for h in range(2):
+                    units.append((fill_rep(n + 1, h), 0, n + 1))
+            if n > 0:
+                for f in side.get(n, []):
+                    units.append((f, zneed["bw"] if n >= 10 else 0, -1))
             if KINDS[n] == "A":
                 for bt in range(NBT):
-                    units.append((fill_arg(order[n], bt), zneed[order[n] // 2]))
+                    units.append((fill_arg(order[n], bt), zneed[order[n] // 2], -1))
+            if n == 0:
+                for f in side[n]:
+                    units.append((f, 0, -1))
+            if n == 0:
+                zneed[1] = zneed[2] = len(units) - 1
+                zneed[3] = zneed[4] = len(units)
+            elif n == 8:
+                zneed["bw"] = len(units) - (NBT if KINDS[n] == "A" else 0)
 
         def side_copy(n):
             if n not in side:
                 return
-            tp = next_unit()
-            if n == 6:
-                nc.scalar.copy(out=zt[:, 3:5, :], in_=tp[:])
-            elif n in (7, 8):
-                nc.vector.tensor_copy(out=bwT[:, 2 * (n - 7) : 2 * (n - 7) + 2, :], in_=tp[:])
-            else:
-                nc.vector.tensor_copy(out=base_sb[:, (n - 10) // 2, :], in_=tp[:])
-            refill()
+            for k in range(len(side[n])):
+                tp = next_unit()
+                if n == 0 and k < 2:
+                    nc.vector.tensor_copy(out=xT[:, 2 * k : 2 * k + 2, :], in_=tp[:])
+                elif n == 0:
+                    nc.scalar.copy(out=zt[:, 2 * k - 3 : 2 * k - 1, :], in_=tp[:])
+                elif n in (7, 8):
+                    nc.vector.tensor_copy(out=bwT[:, 2 * (n - 7) : 2 * (n - 7) + 2, :], in_=tp[:])
+                else:
+                    nc.vector.tensor_copy(out=base_sb[:, (n - 10) // 2, :], in_=tp[:])
+                refill()
 
         make_identity(nc, ident[:])
+        nc.sync.dma_start(out=x0_sb[:], in_=x[:, 0:32].rearrange("(t p) i -> p t i", p=P))
         nc.sync.dma_start(out=gb[:], in_=grid.partition_broadcast(P))
+        w_load(0)
         nc.sync.dma_start(out=x_sb[:], in_=x.rearrange("(t p) i -> p t i", p=P))
-        for n in range(4):
+        for n in range(1, 4):
             w_load(n)
         nc.vector.memset(warm[:], 0.0)
         nc.scalar.activation(out=warm2[:], in_=warm[:], func=ACT.Exp)
-        nc.gpsimd.memset(z[:, :, :, 96:128], 0.0)
+        nc.vector.memset(z0[:, :, :, 96:128], 0.0)
+        nc.gpsimd.memset(zr[:, :, :, 96:128], 0.0)
         nc.vector.memset(alpha[0:32, :], 2.0)
         nc.vector.memset(alpha[32:64, :], 0.0)
         nc.vector.memset(alpha[64:128, :], 0.0)
@@ -338,54 +405,68 @@ def tile_rbfkanlayer_kernel(tc, x, spline_weight, base_weight, grid, out):
         nc.vector.tensor_reduce(
             out=mask[:], in_=ident[:].rearrange("p (a q) -> p q a", q=G), axis=AX.X, op=ALU.add
         )
-        nc.vector.tensor_tensor(out=prod[:], in0=gb[:], in1=mask[:], op=ALU.mult)
+
+        def z_rows(zt_, q_, xs):
+            nc.vector.tensor_tensor(out=q_[:], in0=xs, in1=xs, op=ALU.mult)
+            nc.vector.tensor_copy(out=zt_[:, :, :, 0:32], in_=xs)
+            nc.vector.tensor_copy(out=zt_[:, :, :, 32:64], in_=q_[:])
+            nc.vector.tensor_tensor(
+                out=zt_[:, :, :, 64:96], in0=q_[:], in1=zt_[:, :, :, 32:64], op=ALU.subtract
+            )
+
+        def exponent_weights(h):
+            nc.vector.tensor_tensor(
+                out=lmat[:, 16 * h : 16 * h + 16],
+                in0=mask[:, 16 * h : 16 * h + 16].unsqueeze(2).to_broadcast([P, 16, G]),
+                in1=coef[:].unsqueeze(1).to_broadcast([P, 16, G]),
+                op=ALU.mult,
+            )
+
+        z_rows(z0, q0, x0_sb[:].unsqueeze(2))
         nc.vector.tensor_scalar(
             out=coef[:], in0=gb[:], scalar1=alpha[:], scalar2=beta[:], op0=ALU.mult, op1=ALU.add
         )
+        nc.vector.tensor_tensor(out=prod[:], in0=gb[:], in1=mask[:], op=ALU.mult)
+        exponent_weights(0)
         nc.vector.tensor_reduce(out=gsel[:], in_=prod[:], axis=AX.X, op=ALU.add)
-        nc.vector.tensor_scalar(out=gneg[:], in0=gsel[:], scalar1=-1.0, scalar2=None, op0=ALU.mult)
-        nc.vector.tensor_scalar(out=g2neg[:], in0=gsel[:], scalar1=-2.0, scalar2=None, op0=ALU.mult)
         nc.vector.scalar_tensor_tensor(
             out=gbias[:], in0=gsel[:], scalar=-20.0, in1=gsel[:], op0=ALU.mult, op1=ALU.mult
-        )
-        nc.vector.tensor_tensor(
-            out=lmat[:],
-            in0=mask[:].unsqueeze(2).to_broadcast([P, 32, G]),
-            in1=coef[:].unsqueeze(1).to_broadcast([P, 32, G]),
-            op=ALU.mult,
-        )
-        zx = x_sb[:, :, 0 : 32 * PAIRS].rearrange("p t (r i) -> p t r i", i=32)
-        nc.vector.tensor_tensor(out=q32[:], in0=zx, in1=zx, op=ALU.mult)
-        nc.vector.tensor_copy(out=z[:, :, :, 0:32], in_=zx)
-        nc.vector.tensor_copy(out=z[:, :, :, 32:64], in_=q32[:])
-        nc.vector.tensor_tensor(
-            out=z[:, :, :, 64:96], in0=q32[:], in1=z[:, :, :, 32:64], op=ALU.subtract
         )
         fill_to(4)
         tp = next_unit()
         nc.scalar.copy(out=zt[:, 0:1, :], in_=tp[:])
-        refill()
-        for h in range(2):
-            tp = next_unit()
-            nc.vector.tensor_copy(out=xT[:, 2 * h : 2 * h + 2, :], in_=tp[:])
-            refill()
-        nc.sync.dma_start(out=scratch.rearrange("(f j) b -> j f b", f=FI), in_=xT[:])
-        for k in range(4):
-            x_load(xsteps[k])
-            w_load(4 + k)
-        nc.sync.dma_start(out=bw_sb[:], in_=base_weight.rearrange("(t p) i -> p t i", p=P))
-        for k in range(4, XB):
-            x_load(xsteps[k])
-        tp = next_unit()
-        nc.scalar.copy(out=zt[:, 1:3, :], in_=tp[:])
-        refill()
         w_group(0)
-        w_group(1)
+        exponent_weights(1)
         w_quant(0)
-        w_quant(1)
+        z_rows(zr, qr, x_sb[:, :, 32 : 32 * PAIRS].rearrange("p t (r i) -> p t r i", i=32))
+        refill()
 
         for n in range(NPASS):
             last = n == NPASS - 1
+            if n == 0:
+                pass_exps(0)
+                side_copy(0)
+                nc.sync.dma_start(out=scratch.rearrange("(f j) b -> j f b", f=FI), in_=xT[:])
+                for k in range(4):
+                    x_load(xsteps[k])
+                    w_load(4 + k)
+                nc.sync.dma_start(out=bw_sb[:], in_=base_weight.rearrange("(t p) i -> p t i", p=P))
+                for k in range(4, XB):
+                    x_load(xsteps[k])
+                nc.vector.tensor_scalar(
+                    out=gneg[:], in0=gsel[:], scalar1=-1.0, scalar2=None, op0=ALU.mult
+                )
+                nc.vector.tensor_scalar(
+                    out=g2neg[:], in0=gsel[:], scalar1=-2.0, scalar2=None, op0=ALU.mult
+                )
+                w_group(1)
+                w_quant(1)
+                nc.vector.tensor_copy(
+                    out=xx[:],
+                    in_=x_sb[:, :, 16 * NA : 16 * (NA + NREP)]
+                    .unsqueeze(3)
+                    .to_broadcast([P, NBT, 16 * NREP, 2]),
+                )
             if n + 2 < NPASS:
                 w_group(n + 2)
             if n >= 1:
@@ -395,27 +476,30 @@ def tile_rbfkanlayer_kernel(tc, x, spline_weight, base_weight, grid, out):
                 w_quant(n + 2)
                 if KINDS[n + 2] == "V":
                     squares(n + 2)
+            if n + REP_AHEAD < NPASS and KINDS[n + REP_AHEAD] == "R":
+                repeat_x(n + REP_AHEAD)
             if n + 1 < NPASS and KINDS[n + 1] == "S":
                 squares(n + 1)
-            side_copy(n)
-            if KINDS[n] != "A":
-                exp_sq(n)
-            else:
+            if n + 1 < NPASS and KINDS[n + 1] == "R":
+                squares_r(n + 1)
+            if n > 0 and not last:
+                side_copy(n)
+                pass_exps(n)
+            if last:
                 new_bg(n)
-                if last:
-                    b_tiles(n)
-                    for m in range(n - MX_LAG, n):
-                        for bt in range(NBT):
-                            mx(m, bt)
+                b_tiles(n)
+                for bt in range(NBT):
+                    mx(n - 1, bt)
                 for bt in range(NBT):
                     exp_a_piece(n, bt)
-                    if last:
-                        b_quant(n, bt * P, P)
-                        mx(n, bt)
-                        if bt >= 1:
-                            finish(bt - 1)
-                if last:
-                    finish(NBT - 1)
+                    b_quant(n, bt * P, P)
+                    mx(n, bt)
+                    if bt >= 1:
+                        finish(bt - 1)
+                finish(NBT - 1)
             if n >= MX_LAG and not last:
                 for bt in range(NBT):
                     mx(n - MX_LAG, bt)
+            if n == NPASS - 2:
+                for bt in range(NBT):
+                    mx(n - 1, bt)

@@ -32,7 +32,8 @@ NREP = KINDS.count("R")
 REP_AHEAD = 4
 MX_LAG = 2
 WB = 8
-XB = 7
+XB = 8
+LOADS_AHEAD = 6
 
 
 def pass_order():
@@ -212,8 +213,6 @@ def tile_rbfkanlayer_kernel(tc, x, spline_weight, base_weight, grid, out):
                 in_=wr_t[n][:].rearrange("p t (c i) -> p c t i", i=4),
             )
             wg_t[n] = wg
-            if n + WB < NPASS:
-                w_load(n + WB)
 
         def w_quant(n):
             wc = pool.tile([P, O], U32, align_bytes=64, name="wc", bufs=8)
@@ -234,9 +233,6 @@ def tile_rbfkanlayer_kernel(tc, x, spline_weight, base_weight, grid, out):
                     )
             else:
                 nc.scalar.activation(out=sv, in_=xv, func=ACT.Square, bias=gneg[:], scale=1.0)
-            j = xsteps.index(n) + XB
-            if j < len(xsteps):
-                x_load(xsteps[j])
 
         def repeat_x(n):
             xb = pool.tile([P, NBT, 16, G], BF16, name="xb", bufs=3)
@@ -384,12 +380,22 @@ def tile_rbfkanlayer_kernel(tc, x, spline_weight, base_weight, grid, out):
                     nc.vector.tensor_copy(out=base_sb[:, (n - 10) // 2, :], in_=tp[:])
                 refill()
 
+        due = [(n - 2, 0, n) for n in range(7, NPASS)]
+        due += [(n - (2 if KINDS[n] == "V" else 1), 1, n) for n in xsteps]
+        due = sorted(due)
+
+        def loads_to(step):
+            while due and due[0][0] <= step:
+                entry = due[0]
+                due.remove(entry)
+                (w_load, x_load)[entry[1]](entry[2])
+
         make_identity(nc, ident[:])
         nc.sync.dma_start(out=x0_sb[:], in_=x[:, 0:32].rearrange("(t p) i -> p t i", p=P))
         nc.sync.dma_start(out=gb[:], in_=grid.partition_broadcast(P))
         w_load(0)
         nc.sync.dma_start(out=x_sb[:], in_=x.rearrange("(t p) i -> p t i", p=P))
-        for n in range(1, 4):
+        for n in range(1, 7):
             w_load(n)
         nc.vector.memset(warm[:], 0.0)
         nc.scalar.activation(out=warm2[:], in_=warm[:], func=ACT.Exp)
@@ -447,12 +453,8 @@ def tile_rbfkanlayer_kernel(tc, x, spline_weight, base_weight, grid, out):
                 pass_exps(0)
                 side_copy(0)
                 nc.sync.dma_start(out=scratch.rearrange("(f j) b -> j f b", f=FI), in_=xT[:])
-                for k in range(4):
-                    x_load(xsteps[k])
-                    w_load(4 + k)
+                loads_to(LOADS_AHEAD)
                 nc.sync.dma_start(out=bw_sb[:], in_=base_weight.rearrange("(t p) i -> p t i", p=P))
-                for k in range(4, XB):
-                    x_load(xsteps[k])
                 nc.vector.tensor_scalar(
                     out=gneg[:], in0=gsel[:], scalar1=-1.0, scalar2=None, op0=ALU.mult
                 )
@@ -503,3 +505,4 @@ def tile_rbfkanlayer_kernel(tc, x, spline_weight, base_weight, grid, out):
             if n == NPASS - 2:
                 for bt in range(NBT):
                     mx(n - 1, bt)
+            loads_to(n + 1 + LOADS_AHEAD)

@@ -27,9 +27,9 @@ FLOPS = 2 * B * I * G * O + 2 * B * I * O
 
 NA = 9
 PAIRS = (NA + 1) // 2
-KINDS = "AAAAAA" + "RVSRVSA" * 2 + "RVS" * 3 + "SVA"
+KINDS = "R" + "AAAAAA" + "RVSVRV" + "A" + "SVRVSVRV" + "A" + "SVRVSVRS" + "A"
 NREP = KINDS.count("R")
-REP_AHEAD = 4
+REP_AHEAD = 5
 MX_LAG = 2
 WB = 8
 XB = 8
@@ -62,14 +62,15 @@ def tile_rbfkanlayer_kernel(tc, x, spline_weight, base_weight, grid, out):
         xT = const.tile([P, FI, B], BF16)
         bwT = const.tile([P, FI, O], BF16)
         base_sb = const.tile([P, NBT, O], F32)
-        x0_sb = const.tile([P, NBT, 32], BF16)
+        x0_sb = const.tile([P, NBT, 16], BF16)
+        xx0 = const.tile([P, NBT, 16, 2], BF16)
         z0 = const.tile([P, NBT, 1, P], BF16)
         zr = const.tile([P, NBT, PAIRS - 1, P], BF16)
         q0 = const.tile([P, NBT, 1, 32], F32)
         qr = const.tile([P, NBT, PAIRS - 1, 32], F32)
         zt = const.tile([P, PAIRS, B], BF16)
         lmat = const.tile([P, 32, G], BF16)
-        xx = const.tile([P, NBT, 16 * NREP, 2], BF16)
+        xx = const.tile([P, NBT, 16 * (NREP - 1), 2], BF16)
         mask = const.tile([P, G], F32)
         prod = const.tile([P, G], F32)
         gsel = const.tile([P, 1], F32)
@@ -235,11 +236,11 @@ def tile_rbfkanlayer_kernel(tc, x, spline_weight, base_weight, grid, out):
                 nc.scalar.activation(out=sv, in_=xv, func=ACT.Square, bias=gneg[:], scale=1.0)
 
         def repeat_x(n):
-            xb = pool.tile([P, NBT, 16, G], BF16, name="xb", bufs=3)
-            j = order[n] - NA
+            xb = pool.tile([P, NBT, 16, G], BF16, name="xb", bufs=4)
+            src, j = (xx0, 0) if n == 0 else (xx, order[n] - NA - 1)
             nc.vector.tensor_copy(
                 out=xb[:].rearrange("p t i g -> p (t i g)").bitcast(F32).rearrange("p (t i w) -> p t i w", t=NBT, i=16),
-                in_=xx[:].rearrange("p t i e -> p (t i e)").bitcast(F32).rearrange("p (t i) -> p t i", t=NBT)[
+                in_=src[:].rearrange("p t i e -> p (t i e)").bitcast(F32).rearrange("p (t i) -> p t i", t=NBT)[
                     :, :, 16 * j : 16 * j + 16
                 ].unsqueeze(3).to_broadcast([P, NBT, 16, G // 2]),
             )
@@ -266,13 +267,22 @@ def tile_rbfkanlayer_kernel(tc, x, spline_weight, base_weight, grid, out):
 
         def exp_sq(n):
             bg = new_bg(n)
-            nc.scalar.activation(
-                out=bg[:] if KINDS[n] == "R" else bg[:].rearrange("p (c i) t -> p c t i", i=4),
-                in_=sq_t[n][:],
-                func=ACT.Exp,
-                bias=gbias[:] if KINDS[n] == "V" else 0.0,
-                scale=-20.0,
-            )
+            pieces = NBT if n == NPASS - 2 else 1
+            if pieces > 1:
+                b_tiles(n)
+            for k in range(pieces):
+                w = B // pieces
+                bk = bg[:, k * w : (k + 1) * w, :]
+                nc.scalar.activation(
+                    out=bk if KINDS[n] == "R" else bk.rearrange("p (c i) t -> p c t i", i=4),
+                    in_=sq_t[n][:, k * w : (k + 1) * w] if KINDS[n] == "R" else sq_t[n][:, k * w // 4 : (k + 1) * w // 4],
+                    func=ACT.Exp,
+                    bias=gbias[:] if KINDS[n] == "V" else 0.0,
+                    scale=-20.0,
+                )
+                if pieces > 1:
+                    b_quant(n, k * w, w)
+                    mx(n, k)
 
         def exp_a_piece(n, bt):
             tp = next_unit()
@@ -330,54 +340,56 @@ def tile_rbfkanlayer_kernel(tc, x, spline_weight, base_weight, grid, out):
                 for bt in range(NBT):
                     exp_a_piece(n, bt)
 
-        def finish(bt):
+        def finish(bt, parts):
             res = pool.tile([P, O], F32, name="res", bufs=4)
-            nc.vector.tensor_tensor(out=res[:], in0=acc[bt][:], in1=base_sb[:, bt, :], op=ALU.add)
-            nc.sync.dma_start(out=out[bt * P : (bt + 1) * P, :], in_=res[:])
+            w = O // parts
+            for k in range(parts):
+                cols = slice(k * w, (k + 1) * w)
+                nc.vector.tensor_tensor(
+                    out=res[:, cols], in0=acc[bt][:, cols], in1=base_sb[:, bt, cols], op=ALU.add
+                )
+                nc.sync.dma_start(out=out[bt * P : (bt + 1) * P, cols], in_=res[:, cols])
 
-        units.append((fill_z([0]), 0, -1))
-        zneed = {0: 1}
+        for h in range(2):
+            units.append((fill_rep(0, h), 0, 0))
+        units.append((fill_z([0]), 0, -2))
+        units.append((fill_xT(0), 0, -1))
+        units.append((fill_xT(1), 0, -1))
+        zneed = {0: 3}
         side = {
-            0: [fill_xT(0), fill_xT(1), fill_z([1, 2]), fill_z([3, 4])],
-            7: [fill_bwT(0)],
-            8: [fill_bwT(1)],
-            10: [fill_base(0)],
-            12: [fill_base(1)],
-            14: [fill_base(2)],
-            16: [fill_base(3)],
+            2: [fill_z([1, 2]), fill_z([3, 4])],
+            8: [fill_bwT(0)],
+            10: [fill_bwT(1)],
+            12: [fill_base(0)],
+            15: [fill_base(1)],
+            17: [fill_base(2)],
+            19: [fill_base(3)],
         }
         for n in range(NPASS):
             if n + 1 < NPASS and KINDS[n + 1] == "R":
                 for h in range(2):
                     units.append((fill_rep(n + 1, h), 0, n + 1))
-            if n > 0:
-                for f in side.get(n, []):
-                    units.append((f, zneed["bw"] if n >= 10 else 0, -1))
             if KINDS[n] == "A":
                 for bt in range(NBT):
                     units.append((fill_arg(order[n], bt), zneed[order[n] // 2], -1))
-            if n == 0:
-                for f in side[n]:
-                    units.append((f, 0, -1))
-            if n == 0:
+            for f in side.get(n, []):
+                units.append((f, zneed["bw"] if n > 10 else 0, -1))
+            if n == 2:
                 zneed[1] = zneed[2] = len(units) - 1
                 zneed[3] = zneed[4] = len(units)
-            elif n == 8:
-                zneed["bw"] = len(units) - (NBT if KINDS[n] == "A" else 0)
+            elif n == 10:
+                zneed["bw"] = len(units)
 
         def side_copy(n):
-            if n not in side:
-                return
-            for k in range(len(side[n])):
+            for k in range(len(side.get(n, []))):
                 tp = next_unit()
-                if n == 0 and k < 2:
-                    nc.vector.tensor_copy(out=xT[:, 2 * k : 2 * k + 2, :], in_=tp[:])
-                elif n == 0:
-                    nc.scalar.copy(out=zt[:, 2 * k - 3 : 2 * k - 1, :], in_=tp[:])
-                elif n in (7, 8):
-                    nc.vector.tensor_copy(out=bwT[:, 2 * (n - 7) : 2 * (n - 7) + 2, :], in_=tp[:])
+                if n == 2:
+                    nc.scalar.copy(out=zt[:, 2 * k + 1 : 2 * k + 3, :], in_=tp[:])
+                elif n in (8, 10):
+                    h = (n - 8) // 2
+                    nc.scalar.copy(out=bwT[:, 2 * h : 2 * h + 2, :], in_=tp[:])
                 else:
-                    nc.vector.tensor_copy(out=base_sb[:, (n - 10) // 2, :], in_=tp[:])
+                    nc.scalar.copy(out=base_sb[:, (12, 15, 17, 19).index(n), :], in_=tp[:])
                 refill()
 
         due = [(n - 2, 0, n) for n in range(7, NPASS)]
@@ -391,11 +403,12 @@ def tile_rbfkanlayer_kernel(tc, x, spline_weight, base_weight, grid, out):
                 (w_load, x_load)[entry[1]](entry[2])
 
         make_identity(nc, ident[:])
-        nc.sync.dma_start(out=x0_sb[:], in_=x[:, 0:32].rearrange("(t p) i -> p t i", p=P))
+        nc.sync.dma_start(
+            out=x0_sb[:], in_=x[:, 16 * NA : 16 * NA + 16].rearrange("(t p) i -> p t i", p=P)
+        )
         nc.sync.dma_start(out=gb[:], in_=grid.partition_broadcast(P))
-        w_load(0)
         nc.sync.dma_start(out=x_sb[:], in_=x.rearrange("(t p) i -> p t i", p=P))
-        for n in range(1, 7):
+        for n in range(7):
             w_load(n)
         nc.vector.memset(warm[:], 0.0)
         nc.scalar.activation(out=warm2[:], in_=warm[:], func=ACT.Exp)
@@ -428,20 +441,28 @@ def tile_rbfkanlayer_kernel(tc, x, spline_weight, base_weight, grid, out):
                 op=ALU.mult,
             )
 
-        z_rows(z0, q0, x0_sb[:].unsqueeze(2))
+        nc.vector.tensor_copy(out=xx0[:], in_=x0_sb[:].unsqueeze(3).to_broadcast([P, NBT, 16, 2]))
+        repeat_x(0)
+        nc.vector.tensor_tensor(out=prod[:], in0=gb[:], in1=mask[:], op=ALU.mult)
         nc.vector.tensor_scalar(
             out=coef[:], in0=gb[:], scalar1=alpha[:], scalar2=beta[:], op0=ALU.mult, op1=ALU.add
         )
-        nc.vector.tensor_tensor(out=prod[:], in0=gb[:], in1=mask[:], op=ALU.mult)
-        exponent_weights(0)
         nc.vector.tensor_reduce(out=gsel[:], in_=prod[:], axis=AX.X, op=ALU.add)
+        nc.vector.tensor_scalar(out=gneg[:], in0=gsel[:], scalar1=-1.0, scalar2=None, op0=ALU.mult)
+        z_rows(z0, q0, x_sb[:, :, 0:32].unsqueeze(2))
+        ready.add(-2)
+        squares_r(0)
+        exponent_weights(0)
         nc.vector.scalar_tensor_tensor(
             out=gbias[:], in0=gsel[:], scalar=-20.0, in1=gsel[:], op0=ALU.mult, op1=ALU.mult
         )
-        fill_to(4)
         tp = next_unit()
         nc.scalar.copy(out=zt[:, 0:1, :], in_=tp[:])
         w_group(0)
+        for h in range(2):
+            tp = next_unit()
+            nc.vector.tensor_copy(out=xT[:, 2 * h : 2 * h + 2, :], in_=tp[:])
+        nc.sync.dma_start(out=scratch.rearrange("(f j) b -> j f b", f=FI), in_=xT[:])
         exponent_weights(1)
         w_quant(0)
         z_rows(zr, qr, x_sb[:, :, 32 : 32 * PAIRS].rearrange("p t (r i) -> p t r i", i=32))
@@ -451,13 +472,8 @@ def tile_rbfkanlayer_kernel(tc, x, spline_weight, base_weight, grid, out):
             last = n == NPASS - 1
             if n == 0:
                 pass_exps(0)
-                side_copy(0)
-                nc.sync.dma_start(out=scratch.rearrange("(f j) b -> j f b", f=FI), in_=xT[:])
                 loads_to(LOADS_AHEAD)
                 nc.sync.dma_start(out=bw_sb[:], in_=base_weight.rearrange("(t p) i -> p t i", p=P))
-                nc.vector.tensor_scalar(
-                    out=gneg[:], in0=gsel[:], scalar1=-1.0, scalar2=None, op0=ALU.mult
-                )
                 nc.vector.tensor_scalar(
                     out=g2neg[:], in0=gsel[:], scalar1=-2.0, scalar2=None, op0=ALU.mult
                 )
@@ -465,13 +481,13 @@ def tile_rbfkanlayer_kernel(tc, x, spline_weight, base_weight, grid, out):
                 w_quant(1)
                 nc.vector.tensor_copy(
                     out=xx[:],
-                    in_=x_sb[:, :, 16 * NA : 16 * (NA + NREP)]
+                    in_=x_sb[:, :, 16 * NA + 16 : 16 * (NA + NREP)]
                     .unsqueeze(3)
-                    .to_broadcast([P, NBT, 16 * NREP, 2]),
+                    .to_broadcast([P, NBT, 16 * NREP - 16, 2]),
                 )
             if n + 2 < NPASS:
                 w_group(n + 2)
-            if n >= 1:
+            if 1 <= n < NPASS - 1:
                 b_tiles(n - 1)
                 b_quant(n - 1, 0, B)
             if n + 2 < NPASS:
@@ -484,25 +500,24 @@ def tile_rbfkanlayer_kernel(tc, x, spline_weight, base_weight, grid, out):
                 squares(n + 1)
             if n + 1 < NPASS and KINDS[n + 1] == "R":
                 squares_r(n + 1)
+            if n == NPASS - 2:
+                for k in range(n - MX_LAG, n):
+                    for bt in range(NBT):
+                        mx(k, bt)
             if n > 0 and not last:
-                side_copy(n)
                 pass_exps(n)
+                side_copy(n)
             if last:
                 new_bg(n)
                 b_tiles(n)
-                for bt in range(NBT):
-                    mx(n - 1, bt)
                 for bt in range(NBT):
                     exp_a_piece(n, bt)
                     b_quant(n, bt * P, P)
                     mx(n, bt)
                     if bt >= 1:
-                        finish(bt - 1)
-                finish(NBT - 1)
-            if n >= MX_LAG and not last:
+                        finish(bt - 1, 1)
+                finish(NBT - 1, 2)
+            if MX_LAG <= n < NPASS - 2:
                 for bt in range(NBT):
                     mx(n - MX_LAG, bt)
-            if n == NPASS - 2:
-                for bt in range(NBT):
-                    mx(n - 1, bt)
             loads_to(n + 1 + LOADS_AHEAD)

@@ -27,7 +27,7 @@ FLOPS = 2 * B * I * G * O + 2 * B * I * O
 
 NA = 9
 PAIRS = (NA + 1) // 2
-KINDS = "R" + "AAAAAA" + "RVSVRV" + "A" + "SVRVSVRV" + "A" + "SVRVSVRS" + "A"
+KINDS = "R" + "AAAAAA" + "RVSVSV" + "A" + "RVSVSVRV" + "A" + "SVSVRVSS" + "A"
 NREP = KINDS.count("R")
 REP_AHEAD = 5
 MX_LAG = 2
@@ -208,20 +208,22 @@ def tile_rbfkanlayer_kernel(tc, x, spline_weight, base_weight, grid, out):
             wr_t[n] = wr
 
         def w_group(n):
-            wg = pool.tile([P, O, T], BF16, align_bytes=64, name="wg", bufs=3)
+            if n % 2 == 0:
+                wg_t[n // 2] = pool.tile([P, 2, O, T], BF16, align_bytes=64, name="wg", bufs=2)
             nc.vector.tensor_copy(
-                out=wg[:].rearrange("p (c i) t -> p c t i", i=4),
+                out=wg_t[n // 2][:, n % 2].rearrange("p (c i) t -> p c t i", i=4),
                 in_=wr_t[n][:].rearrange("p t (c i) -> p c t i", i=4),
             )
-            wg_t[n] = wg
 
-        def w_quant(n):
-            wc = pool.tile([P, O], U32, align_bytes=64, name="wc", bufs=8)
-            ws = pool.tile([P, O], U8, align_bytes=64, name="ws", bufs=8)
+        def w_quant(k):
+            wc = pool.tile([P, 2 * O], U32, align_bytes=64, name="wc", bufs=5)
+            ws = pool.tile([P, 2 * O], U8, align_bytes=64, name="ws", bufs=5)
             nc.vector.quantize_mx(
-                out=wc[:].bitcast(FP8X4), scales=ws[:], in_=wg_t[n][:].rearrange("p o t -> p (o t)")
+                out=wc[:].bitcast(FP8X4),
+                scales=ws[:],
+                in_=wg_t[k][:].rearrange("p c o t -> p (c o t)"),
             )
-            wq_t[n] = (wc, ws)
+            wq_t[k] = (wc, ws)
 
         def squares(n):
             sq_t[n] = pool.tile([P, B // 4, T, 4], F32, name="sq", bufs=4)
@@ -238,12 +240,21 @@ def tile_rbfkanlayer_kernel(tc, x, spline_weight, base_weight, grid, out):
         def repeat_x(n):
             xb = pool.tile([P, NBT, 16, G], BF16, name="xb", bufs=4)
             src, j = (xx0, 0) if n == 0 else (xx, order[n] - NA - 1)
-            nc.vector.tensor_copy(
-                out=xb[:].rearrange("p t i g -> p (t i g)").bitcast(F32).rearrange("p (t i w) -> p t i w", t=NBT, i=16),
-                in_=src[:].rearrange("p t i e -> p (t i e)").bitcast(F32).rearrange("p (t i) -> p t i", t=NBT)[
-                    :, :, 16 * j : 16 * j + 16
-                ].unsqueeze(3).to_broadcast([P, NBT, 16, G // 2]),
-            )
+            parts = 2 if n == 0 else 1
+            w = NBT // parts
+            for k in range(parts):
+                tiles = slice(k * w, (k + 1) * w)
+                nc.vector.tensor_copy(
+                    out=xb[:, tiles]
+                    .rearrange("p t i g -> p (t i g)")
+                    .bitcast(F32)
+                    .rearrange("p (t i w) -> p t i w", t=w, i=16),
+                    in_=src[:, tiles]
+                    .rearrange("p t i e -> p t (i e)")
+                    .bitcast(F32)[:, :, 16 * j : 16 * j + 16]
+                    .unsqueeze(3)
+                    .to_broadcast([P, w, 16, G // 2]),
+                )
             xb_t[n] = xb
             ready.add(n)
             refill()
@@ -310,13 +321,14 @@ def tile_rbfkanlayer_kernel(tc, x, spline_weight, base_weight, grid, out):
 
         def mx(n, bt):
             bc, bs = bq_t[n]
-            wc, ws = wq_t[n]
+            wc, ws = wq_t[n // 2]
+            lo = (n % 2) * O
             nc.tensor.matmul_mx(
                 out=acc[bt][:],
                 lhsT=bc[:, bt * P : (bt + 1) * P].bitcast(FP8X4),
                 lhsT_scale=bs[:, bt * P : (bt + 1) * P],
-                rhs=wc[:].bitcast(FP8X4),
-                rhs_scale=ws[:],
+                rhs=wc[:, lo : lo + O].bitcast(FP8X4),
+                rhs_scale=ws[:, lo : lo + O],
                 start=(n == 0),
                 stop=(n == NPASS - 1),
             )
@@ -425,9 +437,7 @@ def tile_rbfkanlayer_kernel(tc, x, spline_weight, base_weight, grid, out):
             out=mask[:], in_=ident[:].rearrange("p (a q) -> p q a", q=G), axis=AX.X, op=ALU.add
         )
 
-        def z_rows(zt_, q_, xs):
-            nc.vector.tensor_tensor(out=q_[:], in0=xs, in1=xs, op=ALU.mult)
-            nc.vector.tensor_copy(out=zt_[:, :, :, 0:32], in_=xs)
+        def z_halves(zt_, q_):
             nc.vector.tensor_copy(out=zt_[:, :, :, 32:64], in_=q_[:])
             nc.vector.tensor_tensor(
                 out=zt_[:, :, :, 64:96], in0=q_[:], in1=zt_[:, :, :, 32:64], op=ALU.subtract
@@ -441,6 +451,9 @@ def tile_rbfkanlayer_kernel(tc, x, spline_weight, base_weight, grid, out):
                 op=ALU.mult,
             )
 
+        xr = x_sb[:, :, 32 : 32 * PAIRS].rearrange("p t (r i) -> p t r i", i=32)
+        nc.scalar.activation(out=qr[:], in_=xr, func=ACT.Square)
+        nc.scalar.copy(out=zr[:, :, :, 0:32], in_=xr)
         nc.vector.tensor_copy(out=xx0[:], in_=x0_sb[:].unsqueeze(3).to_broadcast([P, NBT, 16, 2]))
         repeat_x(0)
         nc.vector.tensor_tensor(out=prod[:], in0=gb[:], in1=mask[:], op=ALU.mult)
@@ -449,7 +462,10 @@ def tile_rbfkanlayer_kernel(tc, x, spline_weight, base_weight, grid, out):
         )
         nc.vector.tensor_reduce(out=gsel[:], in_=prod[:], axis=AX.X, op=ALU.add)
         nc.vector.tensor_scalar(out=gneg[:], in0=gsel[:], scalar1=-1.0, scalar2=None, op0=ALU.mult)
-        z_rows(z0, q0, x_sb[:, :, 0:32].unsqueeze(2))
+        x0 = x_sb[:, :, 0:32].unsqueeze(2)
+        nc.vector.tensor_tensor(out=q0[:], in0=x0, in1=x0, op=ALU.mult)
+        nc.vector.tensor_copy(out=z0[:, :, :, 0:32], in_=x0)
+        z_halves(z0, q0)
         ready.add(-2)
         squares_r(0)
         exponent_weights(0)
@@ -464,8 +480,7 @@ def tile_rbfkanlayer_kernel(tc, x, spline_weight, base_weight, grid, out):
             nc.vector.tensor_copy(out=xT[:, 2 * h : 2 * h + 2, :], in_=tp[:])
         nc.sync.dma_start(out=scratch.rearrange("(f j) b -> j f b", f=FI), in_=xT[:])
         exponent_weights(1)
-        w_quant(0)
-        z_rows(zr, qr, x_sb[:, :, 32 : 32 * PAIRS].rearrange("p t (r i) -> p t r i", i=32))
+        z_halves(zr, qr)
         refill()
 
         for n in range(NPASS):
@@ -478,20 +493,22 @@ def tile_rbfkanlayer_kernel(tc, x, spline_weight, base_weight, grid, out):
                     out=g2neg[:], in0=gsel[:], scalar1=-2.0, scalar2=None, op0=ALU.mult
                 )
                 w_group(1)
-                w_quant(1)
                 nc.vector.tensor_copy(
                     out=xx[:],
                     in_=x_sb[:, :, 16 * NA + 16 : 16 * (NA + NREP)]
                     .unsqueeze(3)
                     .to_broadcast([P, NBT, 16 * NREP - 16, 2]),
                 )
+            if n == 0:
+                w_quant(0)
             if n + 2 < NPASS:
                 w_group(n + 2)
             if 1 <= n < NPASS - 1:
                 b_tiles(n - 1)
                 b_quant(n - 1, 0, B)
             if n + 2 < NPASS:
-                w_quant(n + 2)
+                if n % 2 == 1:
+                    w_quant((n + 1) // 2)
                 if KINDS[n + 2] == "V":
                     squares(n + 2)
             if n + REP_AHEAD < NPASS and KINDS[n + REP_AHEAD] == "R":
@@ -514,8 +531,9 @@ def tile_rbfkanlayer_kernel(tc, x, spline_weight, base_weight, grid, out):
                     exp_a_piece(n, bt)
                     b_quant(n, bt * P, P)
                     mx(n, bt)
-                    if bt >= 1:
-                        finish(bt - 1, 1)
+                    if bt >= 2:
+                        finish(bt - 2, 1)
+                finish(NBT - 2, 1)
                 finish(NBT - 1, 2)
             if MX_LAG <= n < NPASS - 2:
                 for bt in range(NBT):

@@ -27,7 +27,7 @@ FLOPS = 2 * B * I * G * O + 2 * B * I * O
 
 NA = 9
 PAIRS = (NA + 1) // 2
-KINDS = "R" + "AAAAAA" + "RVSVSV" + "A" + "RVSVSVRV" + "A" + "SVSVRVSS" + "A"
+KINDS = "R" + "AAAAAA" + "RVSVRV" + "A" + "SVRVSVRV" + "A" + "SVRVSVRS" + "A"
 NREP = KINDS.count("R")
 REP_AHEAD = 5
 MX_LAG = 2
@@ -226,16 +226,20 @@ def tile_rbfkanlayer_kernel(tc, x, spline_weight, base_weight, grid, out):
             wq_t[k] = (wc, ws)
 
         def squares(n):
-            sq_t[n] = pool.tile([P, B // 4, T, 4], F32, name="sq", bufs=4)
-            sv = sq_t[n][:].rearrange("p c t i -> p t c i")
-            xv = xr_t[n][:].rearrange("p (t c i) -> p t c i", t=T, i=4)
+            sq_t[n] = pool.tile([P, NCOL], F32, name="sq", bufs=4)
             if KINDS[n] == "V":
-                for t in range(T):
-                    nc.vector.scalar_tensor_tensor(
-                        out=sv[:, t], in0=xv[:, t], scalar=g2neg[:], in1=xv[:, t], op0=ALU.add, op1=ALU.mult
-                    )
+                nc.vector.scalar_tensor_tensor(
+                    out=sq_t[n][:],
+                    in0=xr_t[n][:],
+                    scalar=g2neg[:],
+                    in1=xr_t[n][:],
+                    op0=ALU.add,
+                    op1=ALU.mult,
+                )
             else:
-                nc.scalar.activation(out=sv, in_=xv, func=ACT.Square, bias=gneg[:], scale=1.0)
+                nc.scalar.activation(
+                    out=sq_t[n][:], in_=xr_t[n][:], func=ACT.Square, bias=gneg[:], scale=1.0
+                )
 
         def repeat_x(n):
             xb = pool.tile([P, NBT, 16, G], BF16, name="xb", bufs=4)
@@ -286,7 +290,11 @@ def tile_rbfkanlayer_kernel(tc, x, spline_weight, base_weight, grid, out):
                 bk = bg[:, k * w : (k + 1) * w, :]
                 nc.scalar.activation(
                     out=bk if KINDS[n] == "R" else bk.rearrange("p (c i) t -> p c t i", i=4),
-                    in_=sq_t[n][:, k * w : (k + 1) * w] if KINDS[n] == "R" else sq_t[n][:, k * w // 4 : (k + 1) * w // 4],
+                    in_=sq_t[n][:, k * w : (k + 1) * w]
+                    if KINDS[n] == "R"
+                    else sq_t[n][:]
+                    .rearrange("p (t b) -> p t b", t=T)[:, :, k * w : (k + 1) * w]
+                    .rearrange("p t (c i) -> p c t i", i=4),
                     func=ACT.Exp,
                     bias=gbias[:] if KINDS[n] == "V" else 0.0,
                     scale=-20.0,

@@ -27,7 +27,7 @@ FLOPS = 2 * B * I * G * O + 2 * B * I * O
 
 NA = 9
 PAIRS = (NA + 1) // 2
-KINDS = "R" + "AAAAAA" + "RVSVRV" + "A" + "SVRVSVRV" + "A" + "SVRVSVRS" + "A"
+KINDS = "R" + "AAAAAA" + "RVSVRV" + "A" + "SVRWSVRV" + "A" + "SVRVSVRS" + "A"
 NREP = KINDS.count("R")
 REP_AHEAD = 5
 MX_LAG = 2
@@ -37,17 +37,18 @@ LOADS_AHEAD = 6
 
 
 def pass_order():
-    first = {"A": 0, "R": NA, "V": NA + NREP, "S": NA + NREP + KINDS.count("V")}
+    kinds = KINDS.replace("W", "V")
+    first = {"A": 0, "R": NA, "V": NA + NREP, "S": NA + NREP + kinds.count("V")}
     order = []
-    for n, kind in enumerate(KINDS):
-        order.append(first[kind] + KINDS[:n].count(kind))
+    for n, kind in enumerate(kinds):
+        order.append(first[kind] + kinds[:n].count(kind))
     return order
 
 
 def tile_rbfkanlayer_kernel(tc, x, spline_weight, base_weight, grid, out):
     nc = tc.nc
     order = pass_order()
-    xsteps = [n for n in range(NPASS) if KINDS[n] in "SV"]
+    xsteps = [n for n in range(NPASS) if KINDS[n] in "SVW"]
     with ExitStack() as ctx:
         const = ctx.enter_context(tc.tile_pool(name="const", bufs=1))
         pool = ctx.enter_context(tc.tile_pool(name="pool", bufs=1))
@@ -225,20 +226,31 @@ def tile_rbfkanlayer_kernel(tc, x, spline_weight, base_weight, grid, out):
             )
             wq_t[k] = (wc, ws)
 
-        def squares(n):
-            sq_t[n] = pool.tile([P, NCOL], F32, name="sq", bufs=4)
-            if KINDS[n] == "V":
+        def columns(n, on_vector):
+            if KINDS[n] == "W":
+                return slice(0, B // 2) if on_vector else slice(B // 2, B)
+            return slice(0, B)
+
+        def squares(n, on_vector):
+            if n not in sq_t:
+                sq_t[n] = pool.tile([P, T, B], F32, name="sq", bufs=4)
+            cols = columns(n, on_vector)
+            if on_vector:
                 nc.vector.scalar_tensor_tensor(
-                    out=sq_t[n][:],
-                    in0=xr_t[n][:],
+                    out=sq_t[n][:, :, cols],
+                    in0=xr_t[n][:, :, cols],
                     scalar=g2neg[:],
-                    in1=xr_t[n][:],
+                    in1=xr_t[n][:, :, cols],
                     op0=ALU.add,
                     op1=ALU.mult,
                 )
             else:
                 nc.scalar.activation(
-                    out=sq_t[n][:], in_=xr_t[n][:], func=ACT.Square, bias=gneg[:], scale=1.0
+                    out=sq_t[n][:, :, cols],
+                    in_=xr_t[n][:, :, cols],
+                    func=ACT.Square,
+                    bias=gneg[:],
+                    scale=1.0,
                 )
 
         def repeat_x(n):
@@ -280,28 +292,24 @@ def tile_rbfkanlayer_kernel(tc, x, spline_weight, base_weight, grid, out):
             bg_t[n] = pool.tile([P, B, T], BF16, align_bytes=64, name="bg", bufs=4)
             return bg_t[n]
 
+        def exp_sq_columns(n, bg, lo, width):
+            cols = slice(lo, lo + width)
+            bk = bg[:, cols, :]
+            nc.scalar.activation(
+                out=bk if KINDS[n] == "R" else bk.rearrange("p (c i) t -> p c t i", i=4),
+                in_=sq_t[n][:, cols]
+                if KINDS[n] == "R"
+                else sq_t[n][:, :, cols].rearrange("p t (c i) -> p c t i", i=4),
+                func=ACT.Exp,
+                bias=gbias[:] if KINDS[n] == "V" or (KINDS[n] == "W" and lo < B // 2) else 0.0,
+                scale=-20.0,
+            )
+
         def exp_sq(n):
             bg = new_bg(n)
-            pieces = NBT if n == NPASS - 2 else 1
-            if pieces > 1:
-                b_tiles(n)
+            pieces = 2 if KINDS[n] == "W" else 1
             for k in range(pieces):
-                w = B // pieces
-                bk = bg[:, k * w : (k + 1) * w, :]
-                nc.scalar.activation(
-                    out=bk if KINDS[n] == "R" else bk.rearrange("p (c i) t -> p c t i", i=4),
-                    in_=sq_t[n][:, k * w : (k + 1) * w]
-                    if KINDS[n] == "R"
-                    else sq_t[n][:]
-                    .rearrange("p (t b) -> p t b", t=T)[:, :, k * w : (k + 1) * w]
-                    .rearrange("p t (c i) -> p c t i", i=4),
-                    func=ACT.Exp,
-                    bias=gbias[:] if KINDS[n] == "V" else 0.0,
-                    scale=-20.0,
-                )
-                if pieces > 1:
-                    b_quant(n, k * w, w)
-                    mx(n, k)
+                exp_sq_columns(n, bg, k * B // pieces, B // pieces)
 
         def exp_a_piece(n, bt):
             tp = next_unit()
@@ -343,11 +351,11 @@ def tile_rbfkanlayer_kernel(tc, x, spline_weight, base_weight, grid, out):
 
         def x_load(n):
             c = order[n]
-            xr = pool.tile([P, NCOL], BF16, name="xr", bufs=XB)
+            xr = pool.tile([P, T, B], BF16, name="xr", bufs=XB)
             for f in (0, 2, 1, 3):
                 r0 = f * P + 4 * c
                 nc.sync.dma_start(
-                    out=xr[32 * f : 32 * f + 32, :],
+                    out=xr[32 * f : 32 * f + 32].rearrange("p t b -> p (t b)"),
                     in_=scratch[r0 : r0 + 4, :].rearrange("r b -> (r b)").partition_broadcast(32),
                 )
             xr_t[n] = xr
@@ -413,7 +421,7 @@ def tile_rbfkanlayer_kernel(tc, x, spline_weight, base_weight, grid, out):
                 refill()
 
         due = [(n - 2, 0, n) for n in range(7, NPASS)]
-        due += [(n - (2 if KINDS[n] == "V" else 1), 1, n) for n in xsteps]
+        due += [(n - (1 if KINDS[n] == "S" else 2), 1, n) for n in xsteps]
         due = sorted(due)
 
         def loads_to(step):
@@ -491,8 +499,8 @@ def tile_rbfkanlayer_kernel(tc, x, spline_weight, base_weight, grid, out):
         z_halves(zr, qr)
         refill()
 
-        for n in range(NPASS):
-            last = n == NPASS - 1
+        for n in range(NPASS - 1):
+            last = n == NPASS - 2
             if n == 0:
                 pass_exps(0)
                 loads_to(LOADS_AHEAD)
@@ -511,37 +519,39 @@ def tile_rbfkanlayer_kernel(tc, x, spline_weight, base_weight, grid, out):
                 w_quant(0)
             if n + 2 < NPASS:
                 w_group(n + 2)
-            if 1 <= n < NPASS - 1:
+            if n >= 1:
                 b_tiles(n - 1)
                 b_quant(n - 1, 0, B)
             if n + 2 < NPASS:
                 if n % 2 == 1:
                     w_quant((n + 1) // 2)
-                if KINDS[n + 2] == "V":
-                    squares(n + 2)
+                if KINDS[n + 2] in "VW":
+                    squares(n + 2, True)
             if n + REP_AHEAD < NPASS and KINDS[n + REP_AHEAD] == "R":
                 repeat_x(n + REP_AHEAD)
-            if n + 1 < NPASS and KINDS[n + 1] == "S":
-                squares(n + 1)
+            if n + 1 < NPASS and KINDS[n + 1] in "SW":
+                squares(n + 1, False)
             if n + 1 < NPASS and KINDS[n + 1] == "R":
                 squares_r(n + 1)
-            if n == NPASS - 2:
-                for k in range(n - MX_LAG, n):
-                    for bt in range(NBT):
-                        mx(k, bt)
             if n > 0 and not last:
                 pass_exps(n)
                 side_copy(n)
             if last:
-                new_bg(n)
+                for k in range(n - MX_LAG, n):
+                    for bt in range(NBT):
+                        mx(k, bt)
+                bg = new_bg(n)
+                new_bg(n + 1)
                 b_tiles(n)
+                b_tiles(n + 1)
                 for bt in range(NBT):
-                    exp_a_piece(n, bt)
-                    b_quant(n, bt * P, P)
-                    mx(n, bt)
-                    if bt >= 2:
-                        finish(bt - 2, 1)
-                finish(NBT - 2, 1)
+                    exp_sq_columns(n, bg, bt * P, P)
+                    exp_a_piece(n + 1, bt)
+                    for k in (n, n + 1):
+                        b_quant(k, bt * P, P)
+                        mx(k, bt)
+                    if bt >= 1:
+                        finish(bt - 1, 1)
                 finish(NBT - 1, 2)
             if MX_LAG <= n < NPASS - 2:
                 for bt in range(NBT):

@@ -27,7 +27,7 @@ FLOPS = 2 * B * I * G * O + 2 * B * I * O
 
 NA = 9
 PAIRS = (NA + 1) // 2
-KINDS = "R" + "AAAAAA" + "RVSVRV" + "A" + "SVRWSVRV" + "A" + "SVRVSVRS" + "A"
+KINDS = "R" + "AAAAAA" + "RVSVRV" + "A" + "SVRVSVRV" + "A" + "SVRVSVRS" + "A"
 NREP = KINDS.count("R")
 REP_AHEAD = 5
 MX_LAG = 2

from contextlib import ExitStack

import concourse.mybir as mybir
from concourse.masks import make_identity

BF16 = mybir.dt.bfloat16
F32 = mybir.dt.float32
U32 = mybir.dt.uint32
U8 = mybir.dt.uint8
FP8X4 = mybir.dt.float8_e4m3fn_x4
ALU = mybir.AluOpType
ACT = mybir.ActivationFunctionType
AX = mybir.AxisListType

P = 128
B = 512
I = 512
O = 512
G = 32
NBT = B // P
T = 4
FI = 4
NPASS = 32
NCOL = T * B

FLOPS = 2 * B * I * G * O + 2 * B * I * O

NA = 9
PAIRS = (NA + 1) // 2
KINDS = "R" + "AAAAAA" + "RVSVRV" + "A" + "SVRVSVRV" + "A" + "SVRVSVRS" + "A"
NREP = KINDS.count("R")
REP_AHEAD = 5
MX_LAG = 2
WB = 8
XB = 8
LOADS_AHEAD = 6


def pass_order():
    kinds = KINDS.replace("W", "V")
    first = {"A": 0, "R": NA, "V": NA + NREP, "S": NA + NREP + kinds.count("V")}
    order = []
    for n, kind in enumerate(kinds):
        order.append(first[kind] + kinds[:n].count(kind))
    return order


def tile_rbfkanlayer_kernel(tc, x, spline_weight, base_weight, grid, out):
    nc = tc.nc
    order = pass_order()
    xsteps = [n for n in range(NPASS) if KINDS[n] in "SVW"]
    with ExitStack() as ctx:
        const = ctx.enter_context(tc.tile_pool(name="const", bufs=1))
        pool = ctx.enter_context(tc.tile_pool(name="pool", bufs=1))
        psacc = ctx.enter_context(tc.psum_pool(name="psacc", bufs=1))
        psb = ctx.enter_context(tc.psum_pool(name="psb", bufs=1))
        ctx.enter_context(tc.manual_schedule())

        ident = const.tile([P, P], BF16)
        gb = const.tile([P, G], BF16)
        x_sb = const.tile([P, NBT, I], BF16)
        bw_sb = const.tile([P, NBT, I], BF16)
        xT = const.tile([P, FI, B], BF16)
        bwT = const.tile([P, FI, O], BF16)
        base_sb = const.tile([P, NBT, O], F32)
        x0_sb = const.tile([P, NBT, 16], BF16)
        xx0 = const.tile([P, NBT, 16, 2], BF16)
        z0 = const.tile([P, NBT, 1, P], BF16)
        zr = const.tile([P, NBT, PAIRS - 1, P], BF16)
        q0 = const.tile([P, NBT, 1, 32], F32)
        qr = const.tile([P, NBT, PAIRS - 1, 32], F32)
        zt = const.tile([P, PAIRS, B], BF16)
        lmat = const.tile([P, 32, G], BF16)
        xx = const.tile([P, NBT, 16 * (NREP - 1), 2], BF16)
        mask = const.tile([P, G], F32)
        prod = const.tile([P, G], F32)
        gsel = const.tile([P, 1], F32)
        gneg = const.tile([P, 1], F32)
        g2neg = const.tile([P, 1], F32)
        gbias = const.tile([P, 1], F32)
        alpha = const.tile([P, 1], F32)
        beta = const.tile([P, 1], F32)
        coef = const.tile([P, G], F32)
        warm = const.tile([P, 1], F32)
        warm2 = const.tile([P, 1], F32)
        acc = [psacc.tile([P, O], F32, name="acc%d" % bt) for bt in range(NBT)]
        scratch = out.bitcast(BF16)[0 : B // 2].rearrange("r (h b) -> (r h) b", h=2)

        wr_t = {}
        wg_t = {}
        wq_t = {}
        xr_t = {}
        xb_t = {}
        sq_t = {}
        bg_t = {}
        bq_t = {}

        units = []
        filled = []
        used = [0]
        ready = {-1}

        def fill_to(n):
            while (
                len(filled) < min(n, len(units))
                and units[len(filled)][1] <= used[0]
                and units[len(filled)][2] in ready
            ):
                filled.append(units[len(filled)][0](len(filled) % 4))

        def next_unit():
            t = filled[used[0]]
            used[0] += 1
            return t

        def refill():
            fill_to(used[0] + 4)

        def bank(k, shape, dtype):
            return psb.tile(shape, dtype, tag="b%d" % k, name="bk")

        def fill_xT(h):
            def f(k):
                tp = bank(k, [P, 2, 512], BF16)
                for j in range(2):
                    for bt in range(NBT):
                        nc.tensor.transpose(
                            tp[:, j, bt * P : (bt + 1) * P], x_sb[:, bt, 2 * h + j : I : FI], ident[:]
                        )
                return tp

            return f

        def fill_bwT(h):
            def f(k):
                tp = bank(k, [P, 2, 512], BF16)
                for j in range(2):
                    for bt in range(NBT):
                        nc.tensor.transpose(
                            tp[:, j, bt * P : (bt + 1) * P], bw_sb[:, bt, 2 * h + j : I : FI], ident[:]
                        )
                return tp

            return f

        def fill_base(bt):
            def f(k):
                tp = bank(k, [P, O], F32)
                for j in range(FI):
                    nc.tensor.matmul(
                        out=tp[:],
                        lhsT=xT[:, j, bt * P : (bt + 1) * P],
                        rhs=bwT[:, j, :],
                        start=(j == 0),
                        stop=(j == FI - 1),
                    )
                return tp

            return f

        def fill_z(prs):
            def f(k):
                tp = bank(k, [P, len(prs), 512], BF16)
                for j, pr in enumerate(prs):
                    for bt in range(NBT):
                        src = z0[:, bt, 0, :] if pr == 0 else zr[:, bt, pr - 1, :]
                        nc.tensor.transpose(tp[:, j, bt * P : (bt + 1) * P], src, ident[:])
                return tp

            return f

        def fill_rep(n, h):
            def f(k):
                tp = bank(k, [P, T, 256], BF16)
                for t in range(T):
                    for j in range(2):
                        nc.tensor.transpose(
                            tp[:, t, j * P : (j + 1) * P],
                            xb_t[n][:, 2 * h + j, 4 * t : 4 * t + 4, :].rearrange("p f g -> p (f g)"),
                            ident[:],
                        )
                return tp

            return f

        def fill_arg(c, bt):
            def f(k):
                tp = bank(k, [P, T, P], F32)
                for t in range(T):
                    m0 = 16 * (c % 2) + 4 * t
                    nc.tensor.matmul(
                        out=tp[:, t, :],
                        lhsT=lmat[:, m0 : m0 + 4, :].rearrange("p f g -> p (f g)"),
                        rhs=zt[:, c // 2, bt * P : (bt + 1) * P],
                        start=True,
                        stop=True,
                    )
                return tp

            return f

        def w_load(n):
            c = order[n]
            wr = pool.tile([P, T, O], BF16, name="wr", bufs=WB)
            nc.sync.dma_start(
                out=wr[:],
                in_=spline_weight[c * 512 : (c + 1) * 512, :].rearrange("(t p) o -> p t o", t=T),
            )
            wr_t[n] = wr

        def w_group(n):
            if n % 2 == 0:
                wg_t[n // 2] = pool.tile([P, 2, O, T], BF16, align_bytes=64, name="wg", bufs=2)
            nc.vector.tensor_copy(
                out=wg_t[n // 2][:, n % 2].rearrange("p (c i) t -> p c t i", i=4),
                in_=wr_t[n][:].rearrange("p t (c i) -> p c t i", i=4),
            )

        def w_quant(k):
            wc = pool.tile([P, 2 * O], U32, align_bytes=64, name="wc", bufs=5)
            ws = pool.tile([P, 2 * O], U8, align_bytes=64, name="ws", bufs=5)
            nc.vector.quantize_mx(
                out=wc[:].bitcast(FP8X4),
                scales=ws[:],
                in_=wg_t[k][:].rearrange("p c o t -> p (c o t)"),
            )
            wq_t[k] = (wc, ws)

        def columns(n, on_vector):
            if KINDS[n] == "W":
                return slice(0, B // 2) if on_vector else slice(B // 2, B)
            return slice(0, B)

        def squares(n, on_vector):
            if n not in sq_t:
                sq_t[n] = pool.tile([P, T, B], F32, name="sq", bufs=4)
            cols = columns(n, on_vector)
            if on_vector:
                nc.vector.scalar_tensor_tensor(
                    out=sq_t[n][:, :, cols],
                    in0=xr_t[n][:, :, cols],
                    scalar=g2neg[:],
                    in1=xr_t[n][:, :, cols],
                    op0=ALU.add,
                    op1=ALU.mult,
                )
            else:
                nc.scalar.activation(
                    out=sq_t[n][:, :, cols],
                    in_=xr_t[n][:, :, cols],
                    func=ACT.Square,
                    bias=gneg[:],
                    scale=1.0,
                )

        def repeat_x(n):
            xb = pool.tile([P, NBT, 16, G], BF16, name="xb", bufs=4)
            src, j = (xx0, 0) if n == 0 else (xx, order[n] - NA - 1)
            parts = 2 if n == 0 else 1
            w = NBT // parts
            for k in range(parts):
                tiles = slice(k * w, (k + 1) * w)
                nc.vector.tensor_copy(
                    out=xb[:, tiles]
                    .rearrange("p t i g -> p (t i g)")
                    .bitcast(F32)
                    .rearrange("p (t i w) -> p t i w", t=w, i=16),
                    in_=src[:, tiles]
                    .rearrange("p t i e -> p t (i e)")
                    .bitcast(F32)[:, :, 16 * j : 16 * j + 16]
                    .unsqueeze(3)
                    .to_broadcast([P, w, 16, G // 2]),
                )
            xb_t[n] = xb
            ready.add(n)
            refill()

        def squares_r(n):
            sq_t[n] = pool.tile([P, B, T], F32, name="sq", bufs=4)
            for h in range(2):
                tp = next_unit()
                nc.scalar.activation(
                    out=sq_t[n][:, 256 * h : 256 * h + 256, :],
                    in_=tp[:].rearrange("p t b -> p b t"),
                    func=ACT.Square,
                    bias=gneg[:],
                    scale=1.0,
                )
                refill()

        def new_bg(n):
            bg_t[n] = pool.tile([P, B, T], BF16, align_bytes=64, name="bg", bufs=4)
            return bg_t[n]

        def exp_sq_columns(n, bg, lo, width):
            cols = slice(lo, lo + width)
            bk = bg[:, cols, :]
            nc.scalar.activation(
                out=bk if KINDS[n] == "R" else bk.rearrange("p (c i) t -> p c t i", i=4),
                in_=sq_t[n][:, cols]
                if KINDS[n] == "R"
                else sq_t[n][:, :, cols].rearrange("p t (c i) -> p c t i", i=4),
                func=ACT.Exp,
                bias=gbias[:] if KINDS[n] == "V" or (KINDS[n] == "W" and lo < B // 2) else 0.0,
                scale=-20.0,
            )

        def exp_sq(n):
            bg = new_bg(n)
            pieces = 2 if KINDS[n] == "W" else 1
            for k in range(pieces):
                exp_sq_columns(n, bg, k * B // pieces, B // pieces)

        def exp_a_piece(n, bt):
            tp = next_unit()
            nc.scalar.activation(
                out=bg_t[n][:, bt * P : (bt + 1) * P, :],
                in_=tp[:].rearrange("p t b -> p b t"),
                func=ACT.Exp,
                bias=gbias[:],
                scale=20.0,
            )
            refill()

        def b_tiles(n):
            bc = pool.tile([P, B], U32, align_bytes=64, name="bc", bufs=5)
            bs = pool.tile([P, B], U8, align_bytes=64, name="bs", bufs=5)
            bq_t[n] = (bc, bs)

        def b_quant(n, lo, cols):
            bc, bs = bq_t[n]
            nc.vector.quantize_mx(
                out=bc[:, lo : lo + cols].bitcast(FP8X4),
                scales=bs[:, lo : lo + cols],
                in_=bg_t[n][:, lo : lo + cols, :].rearrange("p b t -> p (b t)"),
            )

        def mx(n, bt):
            bc, bs = bq_t[n]
            wc, ws = wq_t[n // 2]
            lo = (n % 2) * O
            nc.tensor.matmul_mx(
                out=acc[bt][:],
                lhsT=bc[:, bt * P : (bt + 1) * P].bitcast(FP8X4),
                lhsT_scale=bs[:, bt * P : (bt + 1) * P],
                rhs=wc[:, lo : lo + O].bitcast(FP8X4),
                rhs_scale=ws[:, lo : lo + O],
                start=(n == 0),
                stop=(n == NPASS - 1),
            )

        def x_load(n):
            c = order[n]
            xr = pool.tile([P, T, B], BF16, name="xr", bufs=XB)
            for f in (0, 2, 1, 3):
                r0 = f * P + 4 * c
                nc.sync.dma_start(
                    out=xr[32 * f : 32 * f + 32].rearrange("p t b -> p (t b)"),
                    in_=scratch[r0 : r0 + 4, :].rearrange("r b -> (r b)").partition_broadcast(32),
                )
            xr_t[n] = xr

        def pass_exps(n):
            if KINDS[n] != "A":
                exp_sq(n)
            else:
                new_bg(n)
                for bt in range(NBT):
                    exp_a_piece(n, bt)

        def finish(bt, parts):
            res = pool.tile([P, O], F32, name="res", bufs=4)
            w = O // parts
            for k in range(parts):
                cols = slice(k * w, (k + 1) * w)
                nc.vector.tensor_tensor(
                    out=res[:, cols], in0=acc[bt][:, cols], in1=base_sb[:, bt, cols], op=ALU.add
                )
                nc.sync.dma_start(out=out[bt * P : (bt + 1) * P, cols], in_=res[:, cols])

        for h in range(2):
            units.append((fill_rep(0, h), 0, 0))
        units.append((fill_z([0]), 0, -2))
        units.append((fill_xT(0), 0, -1))
        units.append((fill_xT(1), 0, -1))
        zneed = {0: 3}
        side = {
            2: [fill_z([1, 2]), fill_z([3, 4])],
            8: [fill_bwT(0)],
            10: [fill_bwT(1)],
            12: [fill_base(0)],
            15: [fill_base(1)],
            17: [fill_base(2)],
            19: [fill_base(3)],
        }
        for n in range(NPASS):
            if n + 1 < NPASS and KINDS[n + 1] == "R":
                for h in range(2):
                    units.append((fill_rep(n + 1, h), 0, n + 1))
            if KINDS[n] == "A":
                for bt in range(NBT):
                    units.append((fill_arg(order[n], bt), zneed[order[n] // 2], -1))
            for f in side.get(n, []):
                units.append((f, zneed["bw"] if n > 10 else 0, -1))
            if n == 2:
                zneed[1] = zneed[2] = len(units) - 1
                zneed[3] = zneed[4] = len(units)
            elif n == 10:
                zneed["bw"] = len(units)

        def side_copy(n):
            for k in range(len(side.get(n, []))):
                tp = next_unit()
                if n == 2:
                    nc.scalar.copy(out=zt[:, 2 * k + 1 : 2 * k + 3, :], in_=tp[:])
                elif n in (8, 10):
                    h = (n - 8) // 2
                    nc.scalar.copy(out=bwT[:, 2 * h : 2 * h + 2, :], in_=tp[:])
                else:
                    nc.scalar.copy(out=base_sb[:, (12, 15, 17, 19).index(n), :], in_=tp[:])
                refill()

        due = [(n - 2, 0, n) for n in range(7, NPASS)]
        due += [(n - (1 if KINDS[n] == "S" else 2), 1, n) for n in xsteps]
        due = sorted(due)

        def loads_to(step):
            while due and due[0][0] <= step:
                entry = due[0]
                due.remove(entry)
                (w_load, x_load)[entry[1]](entry[2])

        make_identity(nc, ident[:])
        nc.sync.dma_start(
            out=x0_sb[:], in_=x[:, 16 * NA : 16 * NA + 16].rearrange("(t p) i -> p t i", p=P)
        )
        nc.sync.dma_start(out=gb[:], in_=grid.partition_broadcast(P))
        nc.sync.dma_start(out=x_sb[:], in_=x.rearrange("(t p) i -> p t i", p=P))
        for n in range(7):
            w_load(n)
        nc.vector.memset(warm[:], 0.0)
        nc.scalar.activation(out=warm2[:], in_=warm[:], func=ACT.Exp)
        nc.vector.memset(z0[:, :, :, 96:128], 0.0)
        nc.gpsimd.memset(zr[:, :, :, 96:128], 0.0)
        nc.vector.memset(alpha[0:32, :], 2.0)
        nc.vector.memset(alpha[32:64, :], 0.0)
        nc.vector.memset(alpha[64:128, :], 0.0)
        nc.vector.memset(beta[0:32, :], 0.0)
        nc.vector.memset(beta[32:64, :], -1.0)
        nc.vector.memset(beta[64:96, :], -1.0)
        nc.vector.memset(beta[96:128, :], 0.0)
        nc.vector.tensor_reduce(
            out=mask[:], in_=ident[:].rearrange("p (a q) -> p q a", q=G), axis=AX.X, op=ALU.add
        )

        def z_halves(zt_, q_):
            nc.vector.tensor_copy(out=zt_[:, :, :, 32:64], in_=q_[:])
            nc.vector.tensor_tensor(
                out=zt_[:, :, :, 64:96], in0=q_[:], in1=zt_[:, :, :, 32:64], op=ALU.subtract
            )

        def exponent_weights(h):
            nc.vector.tensor_tensor(
                out=lmat[:, 16 * h : 16 * h + 16],
                in0=mask[:, 16 * h : 16 * h + 16].unsqueeze(2).to_broadcast([P, 16, G]),
                in1=coef[:].unsqueeze(1).to_broadcast([P, 16, G]),
                op=ALU.mult,
            )

        xr = x_sb[:, :, 32 : 32 * PAIRS].rearrange("p t (r i) -> p t r i", i=32)
        nc.scalar.activation(out=qr[:], in_=xr, func=ACT.Square)
        nc.scalar.copy(out=zr[:, :, :, 0:32], in_=xr)
        nc.vector.tensor_copy(out=xx0[:], in_=x0_sb[:].unsqueeze(3).to_broadcast([P, NBT, 16, 2]))
        repeat_x(0)
        nc.vector.tensor_tensor(out=prod[:], in0=gb[:], in1=mask[:], op=ALU.mult)
        nc.vector.tensor_scalar(
            out=coef[:], in0=gb[:], scalar1=alpha[:], scalar2=beta[:], op0=ALU.mult, op1=ALU.add
        )
        nc.vector.tensor_reduce(out=gsel[:], in_=prod[:], axis=AX.X, op=ALU.add)
        nc.vector.tensor_scalar(out=gneg[:], in0=gsel[:], scalar1=-1.0, scalar2=None, op0=ALU.mult)
        x0 = x_sb[:, :, 0:32].unsqueeze(2)
        nc.vector.tensor_tensor(out=q0[:], in0=x0, in1=x0, op=ALU.mult)
        nc.vector.tensor_copy(out=z0[:, :, :, 0:32], in_=x0)
        z_halves(z0, q0)
        ready.add(-2)
        squares_r(0)
        exponent_weights(0)
        nc.vector.scalar_tensor_tensor(
            out=gbias[:], in0=gsel[:], scalar=-20.0, in1=gsel[:], op0=ALU.mult, op1=ALU.mult
        )
        tp = next_unit()
        nc.scalar.copy(out=zt[:, 0:1, :], in_=tp[:])
        w_group(0)
        for h in range(2):
            tp = next_unit()
            nc.vector.tensor_copy(out=xT[:, 2 * h : 2 * h + 2, :], in_=tp[:])
        nc.sync.dma_start(out=scratch.rearrange("(f j) b -> j f b", f=FI), in_=xT[:])
        exponent_weights(1)
        z_halves(zr, qr)
        refill()

        for n in range(NPASS - 1):
            last = n == NPASS - 2
            if n == 0:
                pass_exps(0)
                loads_to(LOADS_AHEAD)
                nc.sync.dma_start(out=bw_sb[:], in_=base_weight.rearrange("(t p) i -> p t i", p=P))
                nc.vector.tensor_scalar(
                    out=g2neg[:], in0=gsel[:], scalar1=-2.0, scalar2=None, op0=ALU.mult
                )
                w_group(1)
                nc.vector.tensor_copy(
                    out=xx[:],
                    in_=x_sb[:, :, 16 * NA + 16 : 16 * (NA + NREP)]
                    .unsqueeze(3)
                    .to_broadcast([P, NBT, 16 * NREP - 16, 2]),
                )
            if n == 0:
                w_quant(0)
            if n + 2 < NPASS:
                w_group(n + 2)
            if n >= 1:
                b_tiles(n - 1)
                b_quant(n - 1, 0, B)
            if n + 2 < NPASS:
                if n % 2 == 1:
                    w_quant((n + 1) // 2)
                if KINDS[n + 2] in "VW":
                    squares(n + 2, True)
            if n + REP_AHEAD < NPASS and KINDS[n + REP_AHEAD] == "R":
                repeat_x(n + REP_AHEAD)
            if n + 1 < NPASS and KINDS[n + 1] in "SW":
                squares(n + 1, False)
            if n + 1 < NPASS and KINDS[n + 1] == "R":
                squares_r(n + 1)
            if n > 0 and not last:
                pass_exps(n)
                side_copy(n)
            if last:
                for k in range(n - MX_LAG, n):
                    for bt in range(NBT):
                        mx(k, bt)
                bg = new_bg(n)
                new_bg(n + 1)
                b_tiles(n)
                b_tiles(n + 1)
                for bt in range(NBT):
                    exp_sq_columns(n, bg, bt * P, P)
                    exp_a_piece(n + 1, bt)
                    for k in (n, n + 1):
                        b_quant(k, bt * P, P)
                        mx(k, bt)
                    if bt >= 1:
                        finish(bt - 1, 1)
                finish(NBT - 1, 2)
            if MX_LAG <= n < NPASS - 2:
                for bt in range(NBT):
                    mx(n - MX_LAG, bt)
            loads_to(n + 1 + LOADS_AHEAD)
